import numpy as np
import ml_dtypes


def mxq(x, axis, fmt="e4m3"):
    dtype, down = {"e4m3": (ml_dtypes.float8_e4m3fn, 7), "e5m2": (ml_dtypes.float8_e5m2, 14)}[fmt]
    v = np.moveaxis(np.asarray(x, np.float32).astype(ml_dtypes.bfloat16).astype(np.float64), axis, -1)
    blocks = v.reshape(v.shape[:-1] + (-1, 32))
    amax = np.abs(blocks).max(-1, keepdims=True)
    byte = np.maximum(np.where(amax > 0, np.frexp(amax)[1] - 1 + 127, 0) - down, 1)
    scale = np.exp2(byte - 127.0)
    codes = (blocks / scale).astype(np.float32).astype(dtype).astype(np.float64)
    return np.moveaxis((codes * scale).reshape(v.shape), -1, axis)


WIDE = False


def mx_kscale(k):
    if not WIDE:
        return np.ones(k)
    levels = np.array([10, -10, 5, -5, 0])
    a = np.random.permutation(np.resize(levels, k // 512 * 4)).reshape(k // 512, 4)
    idx = np.arange(k)
    return np.exp2(a[idx // 512, idx % 128 // 32])


BF16 = ml_dtypes.bfloat16


def bf(x):
    return np.asarray(x, np.float32).astype(BF16)


def f64(x):
    return np.asarray(x).astype(np.float64)


B, S, D, H, HD, F = 2, 320, 1024, 16, 64, 4096
E = H * HD
CURV = 1.0


def lift(space):
    t = np.sqrt(np.sum(space * space, -1, keepdims=True) + 1.0 / CURV)
    return np.concatenate([t, space], -1)


def setup_inputs():
    s = mx_kscale(D)
    return {"x_space": bf(np.random.standard_normal((B, S, D)) * 2.0 / np.sqrt(D)),
            "ln1_w": bf((1.0 + 0.1 * np.random.standard_normal(D)) * s),
            "wq": bf(np.random.standard_normal((D, E)) * 0.5 / np.sqrt(D) / s[:, None]),
            "wk": bf(np.random.standard_normal((D, E)) * 0.5 / np.sqrt(D) / s[:, None]),
            "wv": bf(np.random.standard_normal((D, E)) * 0.25 / np.sqrt(D) / s[:, None])}


def reference(x_space, ln1_w, wq, wk, wv):
    s = f64(x_space)
    rms = np.sqrt(np.mean(s * s, -1, keepdims=True) + 1e-6)
    nq = mxq(s / rms * f64(ln1_w), 2, "e4m3")
    q = lift((nq @ mxq(f64(wq), 0, "e4m3")).reshape(B, S, H, HD))
    k = lift((nq @ mxq(f64(wk), 0, "e4m3")).reshape(B, S, H, HD))
    v = lift((nq @ mxq(f64(wv), 0, "e4m3")).reshape(B, S, H, HD))
    return q, k, v

@@ -1,0 +1,275 @@
+from contextlib import ExitStack
+
+import concourse.mybir as mybir
+from concourse.masks import make_identity
+
+F32 = mybir.dt.float32
+BF16 = mybir.dt.bfloat16
+U32 = mybir.dt.uint32
+U8 = mybir.dt.uint8
+FP8X4 = mybir.dt.float8_e4m3fn_x4
+ACT = mybir.ActivationFunctionType
+ALU = mybir.AluOpType
+
+P = 128
+PACK = 4
+K_PASS = P * PACK
+TOKENS = 2 * 320
+D = 1024
+E = 1024
+H = 16
+HD = 64
+EPS = 1e-6
+CURV = 1.0
+PASSES = D // K_PASS
+TOKEN_TILES = TOKENS // P
+N_TILE = 512
+HALVES = E // N_TILE
+HEADS_PER_BANK = N_TILE // HD
+RUN = 4
+
+UNITS = PASSES * HALVES
+VECTOR_COLS = 192
+
+FLOPS = 2 * TOKENS * D * 3 * E
+
+
+def tile_ltransformerdecoderblock_pa_kernel(
+    tc, x_space, ln1_w, wq, wk, wv, out_0, out_1, out_2
+):
+    nc = tc.nc
+    weights = (wq, wk, wv)
+    outputs = [o.rearrange("b s h c -> (b s) (h c)") for o in (out_0, out_1, out_2)]
+    x_rows = x_space.flatten_outer_dims()
+
+    with ExitStack() as ctx:
+        consts = ctx.enter_context(tc.tile_pool(name="consts", bufs=1))
+        xwork = ctx.enter_context(tc.tile_pool(name="xwork", bufs=2))
+        wwork = ctx.enter_context(tc.tile_pool(name="wwork", bufs=4))
+        opool = ctx.enter_context(tc.tile_pool(name="opool", bufs=6))
+        psum = ctx.enter_context(tc.psum_pool(name="psum", bufs=8))
+        ctx.enter_context(tc.manual_schedule())
+
+        one = consts.tile([P, 1], F32)
+        nc.vector.memset(one[:], 1.0)
+        warm = consts.tile([P, 1], F32)
+        nc.scalar.activation(out=warm[:], in_=one[:], func=ACT.Sqrt)
+
+        ident = consts.tile([P, P], F32)
+        make_identity(nc, ident[:])
+
+        gain = consts.tile([P, PASSES, PACK], BF16)
+        nc.scalar.dma_start(
+            out=gain[:], in_=ln1_w.rearrange("(g p t) -> p g t", g=PASSES, t=PACK)
+        )
+
+        x_sb = []
+        raw = []
+
+        def load_tokens(m):
+            x_tile = consts.tile([P, D], BF16, name="x%d" % m)
+            nc.sync.dma_start(out=x_tile[:], in_=x_rows[m * P : (m + 1) * P, :])
+            x_sb.append(x_tile)
+
+        def load_chunk(w, g):
+            raw_tile = consts.tile([P, PACK, E], BF16, name="raw%d_%d" % (w, g))
+            nc.sync.dma_start(
+                out=raw_tile[:],
+                in_=weights[w][g * K_PASS : (g + 1) * K_PASS, :].rearrange(
+                    "(p j) n -> p j n", j=PACK
+                ),
+            )
+            raw.append(raw_tile)
+
+        load_tokens(0)
+        load_tokens(1)
+        load_chunk(0, 0)
+        for m in range(2, TOKEN_TILES):
+            load_tokens(m)
+        load_chunk(0, 1)
+        for w in range(1, len(weights)):
+            for g in range(PASSES):
+                load_chunk(w, g)
+
+        rms = {}
+        rstd = {}
+        xt = {}
+        xg = {}
+        x_codes = {}
+        x_scales = {}
+
+        def sum_squares(m):
+            squares = xwork.tile([P, D], BF16)
+            sumsq = consts.tile([P, 1], F32, name="sumsq%d" % m)
+            nc.scalar.activation(
+                out=squares[:], in_=x_sb[m][:], func=ACT.Square, accum_out=sumsq[:]
+            )
+            rms[m] = consts.tile([P, 1], F32, name="rms%d" % m)
+            nc.scalar.activation(
+                out=rms[m][:], in_=sumsq[:], func=ACT.Sqrt, scale=1.0 / D, bias=EPS
+            )
+
+        def reciprocal(m):
+            rstd[m] = consts.tile([P, 1], F32, name="rstd%d" % m)
+            nc.vector.reciprocal(out=rstd[m][:], in_=rms[m][:])
+
+        def scale_transpose(m):
+            xs = xwork.tile([P, PASSES, PACK, P], F32)
+            nc.scalar.activation(
+                out=xs[:],
+                in_=x_sb[m][:].rearrange("p (g c t) -> p g t c", g=PASSES, t=PACK),
+                func=ACT.Copy,
+                scale=rstd[m][:],
+            )
+            for g in range(PASSES):
+                xt[(m, g)] = psum.tile([P, PACK, P], F32, tag="bank", name="xt")
+                for t in range(PACK):
+                    nc.tensor.transpose(xt[(m, g)][:, t, :], xs[:, g, t, :], ident[:])
+
+        def apply_gain(m):
+            xg[m] = xwork.tile([P, PASSES, P, PACK], BF16, align_bytes=64, name="xg")
+            for g in range(PASSES):
+                nc.vector.tensor_tensor(
+                    out=xg[m][:, g, :, :],
+                    in0=xt[(m, g)][:].rearrange("p t r -> p r t"),
+                    in1=gain[:, g, :].unsqueeze(1).to_broadcast([P, P, PACK]),
+                    op=ALU.mult,
+                )
+
+        def quantise_tokens(m):
+            x_codes[m] = consts.tile([P, PASSES * P], U32, name="xc%d" % m, align_bytes=64)
+            x_scales[m] = consts.tile([P, PASSES * P], U8, name="xsc%d" % m, align_bytes=64)
+            nc.vector.quantize_mx(
+                out=x_codes[m][:].bitcast(FP8X4),
+                scales=x_scales[m][:],
+                in_=xg[m][:].rearrange("p g r t -> p (g r t)"),
+            )
+
+        wg = {}
+        w_codes = {}
+        w_scales = {}
+
+        def regroup(w, u, vector_cols):
+            g, h = divmod(u, HALVES)
+            wg[(w, u)] = wwork.tile([P, N_TILE, PACK], BF16, align_bytes=64, name="wg")
+            dst = wg[(w, u)][:].rearrange("p (c i) t -> p c t i", i=RUN)
+            src = raw[w * PASSES + g][:, :, h * N_TILE : (h + 1) * N_TILE].rearrange(
+                "p t (c i) -> p c t i", i=RUN
+            )
+            split = vector_cols // RUN
+            nc.vector.tensor_copy(out=dst[:, :split], in_=src[:, :split])
+            if vector_cols < N_TILE:
+                nc.scalar.copy(out=dst[:, split:], in_=src[:, split:])
+
+        def quantise_unit(w, u):
+            w_codes[(w, u)] = consts.tile(
+                [P, N_TILE], U32, name="wc%d_%d" % (w, u), align_bytes=64
+            )
+            w_scales[(w, u)] = consts.tile(
+                [P, N_TILE], U8, name="wsc%d_%d" % (w, u), align_bytes=64
+            )
+            nc.vector.quantize_mx(
+                out=w_codes[(w, u)][:].bitcast(FP8X4),
+                scales=w_scales[(w, u)][:],
+                in_=wg[(w, u)][:].rearrange("p n t -> p (n t)"),
+            )
+
+        acc = {}
+        o_sb = {}
+        stats = {}
+        head_sumsq = {}
+
+        def matmuls(w, m):
+            for h in range(HALVES):
+                acc[(w, m, h)] = psum.tile([P, N_TILE], F32, tag="bank", name="acc")
+                for g in range(PASSES):
+                    nc.tensor.matmul_mx(
+                        out=acc[(w, m, h)][:],
+                        lhsT=x_codes[m][:, g * P : (g + 1) * P].bitcast(FP8X4),
+                        lhsT_scale=x_scales[m][:, g * P : (g + 1) * P],
+                        rhs=w_codes[(w, g * HALVES + h)][:].bitcast(FP8X4),
+                        rhs_scale=w_scales[(w, g * HALVES + h)][:],
+                        start=(g == 0),
+                        stop=(g == PASSES - 1),
+                    )
+
+        def evacuate(w, m):
+            o_sb[(w, m)] = opool.tile([P, H, HD + 1], F32, name="o_sb")
+            stats[(w, m)] = opool.tile([P, H, 3], F32, name="stats")
+            for h in range(HALVES):
+                bank = acc[(w, m, h)]
+                first = h * HEADS_PER_BANK
+                nc.scalar.copy(
+                    out=o_sb[(w, m)][:, first : first + HEADS_PER_BANK, 1:],
+                    in_=bank[:].rearrange("p (a c) -> p a c", c=HD),
+                )
+                for j in range(HEADS_PER_BANK // 2):
+                    nc.vector.bn_stats(
+                        out=stats[(w, m)][:, first + 2 * j : first + 2 * j + 2, :].rearrange(
+                            "p a s -> p (a s)"
+                        ),
+                        in_=bank[:, 2 * j * HD : (2 * j + 2) * HD].rearrange(
+                            "p (a c) -> p c a", a=2
+                        ),
+                    )
+
+        def sum_heads(w, m):
+            mean_sq = opool.tile([P, H], F32)
+            nc.vector.tensor_tensor(
+                out=mean_sq[:], in0=stats[(w, m)][:, :, 1], in1=stats[(w, m)][:, :, 1], op=ALU.mult
+            )
+            head_sumsq[(w, m)] = opool.tile([P, H], F32, name="head_sumsq")
+            nc.vector.scalar_tensor_tensor(
+                out=head_sumsq[(w, m)][:],
+                in0=mean_sq[:],
+                scalar=float(HD),
+                in1=stats[(w, m)][:, :, 2],
+                op0=ALU.mult,
+                op1=ALU.add,
+            )
+
+        def lift_and_store(w, m):
+            nc.scalar.activation(
+                out=o_sb[(w, m)][:, :, 0], in_=head_sumsq[(w, m)][:], func=ACT.Sqrt, bias=1.0 / CURV
+            )
+            nc.sync.dma_start(
+                out=outputs[w][m * P : (m + 1) * P, :],
+                in_=o_sb[(w, m)][:].rearrange("p h c -> p (h c)"),
+            )
+
+        sum_squares(0)
+        reciprocal(0)
+        sum_squares(1)
+        reciprocal(1)
+        scale_transpose(0)
+        for m in range(TOKEN_TILES):
+            if m < UNITS:
+                regroup(0, m, N_TILE)
+            if m + 2 < TOKEN_TILES:
+                sum_squares(m + 2)
+            if m + 1 < TOKEN_TILES:
+                scale_transpose(m + 1)
+            apply_gain(m)
+            if m + 2 < TOKEN_TILES:
+                reciprocal(m + 2)
+            if m < UNITS:
+                quantise_unit(0, m)
+            quantise_tokens(m)
+
+        steps = [(w, m) for w in range(len(weights)) for m in range(TOKEN_TILES)]
+        matmuls(0, 0)
+        for i, (w, m) in enumerate(steps):
+            prepare = w + 1 < len(weights) and m < UNITS
+            if i + 1 < len(steps):
+                matmuls(steps[i + 1][0], steps[i + 1][1])
+            if i > 0:
+                sum_heads(steps[i - 1][0], steps[i - 1][1])
+            if prepare:
+                regroup(w + 1, m, VECTOR_COLS)
+            evacuate(w, m)
+            if i > 0:
+                lift_and_store(steps[i - 1][0], steps[i - 1][1])
+            if prepare:
+                quantise_unit(w + 1, m)
+        sum_heads(steps[-1][0], steps[-1][1])
+        lift_and_store(steps[-1][0], steps[-1][1])

@@ -26,10 +26,11 @@ TOKEN_TILES = TOKENS // P
 N_TILE = 512
 HALVES = E // N_TILE
 HEADS_PER_BANK = N_TILE // HD
-RUN = 4
-
 UNITS = PASSES * HALVES
+RUN = 4
 VECTOR_COLS = 192
+SCALAR_AHEAD = 2
+VECTOR_AHEAD = 1
 
 FLOPS = 2 * TOKENS * D * 3 * E
 
@@ -63,35 +64,32 @@ def tile_ltransformerdecoderblock_pa_kernel(
             out=gain[:], in_=ln1_w.rearrange("(g p t) -> p g t", g=PASSES, t=PACK)
         )
 
-        x_sb = []
-        raw = []
+        x_sb = {}
+        raw = {}
 
         def load_tokens(m):
-            x_tile = consts.tile([P, D], BF16, name="x%d" % m)
-            nc.sync.dma_start(out=x_tile[:], in_=x_rows[m * P : (m + 1) * P, :])
-            x_sb.append(x_tile)
+            x_sb[m] = consts.tile([P, D], BF16, name="x%d" % m)
+            nc.sync.dma_start(out=x_sb[m][:], in_=x_rows[m * P : (m + 1) * P, :])
 
-        def load_chunk(w, g):
-            raw_tile = consts.tile([P, PACK, E], BF16, name="raw%d_%d" % (w, g))
+        def load_unit(w, u):
+            g, h = divmod(u, HALVES)
+            raw[(w, u)] = consts.tile([P, PACK, N_TILE], BF16, name="raw%d_%d" % (w, u))
             nc.sync.dma_start(
-                out=raw_tile[:],
-                in_=weights[w][g * K_PASS : (g + 1) * K_PASS, :].rearrange(
-                    "(p j) n -> p j n", j=PACK
-                ),
+                out=raw[(w, u)][:],
+                in_=weights[w][
+                    g * K_PASS : (g + 1) * K_PASS, h * N_TILE : (h + 1) * N_TILE
+                ].rearrange("(p j) n -> p j n", j=PACK),
             )
-            raw.append(raw_tile)
 
-        load_tokens(0)
-        load_tokens(1)
-        load_chunk(0, 0)
-        for m in range(2, TOKEN_TILES):
+        for m in range(TOKEN_TILES):
             load_tokens(m)
-        load_chunk(0, 1)
-        for w in range(1, len(weights)):
-            for g in range(PASSES):
-                load_chunk(w, g)
+            if m < UNITS:
+                load_unit(0, m)
+        later_units = [(w, u) for w in range(1, len(weights)) for u in range(UNITS)]
+        for w, u in later_units:
+            load_unit(w, u)
 
-        rms = {}
+        sumsq = {}
         rstd = {}
         xt = {}
         xg = {}
@@ -100,13 +98,17 @@ def tile_ltransformerdecoderblock_pa_kernel(
 
         def sum_squares(m):
             squares = xwork.tile([P, D], BF16)
-            sumsq = consts.tile([P, 1], F32, name="sumsq%d" % m)
+            sumsq[m] = consts.tile([P, 1], F32, name="sumsq%d" % m)
             nc.scalar.activation(
-                out=squares[:], in_=x_sb[m][:], func=ACT.Square, accum_out=sumsq[:]
+                out=squares[:], in_=x_sb[m][:], func=ACT.Square, accum_out=sumsq[m][:]
             )
+
+        rms = {}
+
+        def root_mean_square(m):
             rms[m] = consts.tile([P, 1], F32, name="rms%d" % m)
             nc.scalar.activation(
-                out=rms[m][:], in_=sumsq[:], func=ACT.Sqrt, scale=1.0 / D, bias=EPS
+                out=rms[m][:], in_=sumsq[m][:], func=ACT.Sqrt, scale=1.0 / D, bias=EPS
             )
 
         def reciprocal(m):
@@ -149,17 +151,20 @@ def tile_ltransformerdecoderblock_pa_kernel(
         w_codes = {}
         w_scales = {}
 
-        def regroup(w, u, vector_cols):
-            g, h = divmod(u, HALVES)
-            wg[(w, u)] = wwork.tile([P, N_TILE, PACK], BF16, align_bytes=64, name="wg")
+        def regroup_views(w, u):
+            if (w, u) not in wg:
+                wg[(w, u)] = wwork.tile([P, N_TILE, PACK], BF16, align_bytes=64, name="wg")
             dst = wg[(w, u)][:].rearrange("p (c i) t -> p c t i", i=RUN)
-            src = raw[w * PASSES + g][:, :, h * N_TILE : (h + 1) * N_TILE].rearrange(
-                "p t (c i) -> p c t i", i=RUN
-            )
-            split = vector_cols // RUN
-            nc.vector.tensor_copy(out=dst[:, :split], in_=src[:, :split])
-            if vector_cols < N_TILE:
-                nc.scalar.copy(out=dst[:, split:], in_=src[:, split:])
+            src = raw[(w, u)][:].rearrange("p t (c i) -> p c t i", i=RUN)
+            return dst, src
+
+        def regroup_vector(w, u, cols):
+            dst, src = regroup_views(w, u)
+            nc.vector.tensor_copy(out=dst[:, : cols // RUN], in_=src[:, : cols // RUN])
+
+        def regroup_scalar(w, u, cols):
+            dst, src = regroup_views(w, u)
+            nc.scalar.copy(out=dst[:, cols // RUN :], in_=src[:, cols // RUN :])
 
         def quantise_unit(w, u):
             w_codes[(w, u)] = consts.tile(
@@ -193,22 +198,23 @@ def tile_ltransformerdecoderblock_pa_kernel(
                         stop=(g == PASSES - 1),
                     )
 
-        def evacuate(w, m):
+        def copy_out(w, m):
             o_sb[(w, m)] = opool.tile([P, H, HD + 1], F32, name="o_sb")
-            stats[(w, m)] = opool.tile([P, H, 3], F32, name="stats")
             for h in range(HALVES):
-                bank = acc[(w, m, h)]
                 first = h * HEADS_PER_BANK
                 nc.scalar.copy(
                     out=o_sb[(w, m)][:, first : first + HEADS_PER_BANK, 1:],
-                    in_=bank[:].rearrange("p (a c) -> p a c", c=HD),
+                    in_=acc[(w, m, h)][:].rearrange("p (a c) -> p a c", c=HD),
                 )
+
+        def head_stats(w, m):
+            stats[(w, m)] = opool.tile([P, H, 3], F32, name="stats")
+            for h in range(HALVES):
                 for j in range(HEADS_PER_BANK // 2):
+                    first = h * HEADS_PER_BANK + 2 * j
                     nc.vector.bn_stats(
-                        out=stats[(w, m)][:, first + 2 * j : first + 2 * j + 2, :].rearrange(
-                            "p a s -> p (a s)"
-                        ),
-                        in_=bank[:, 2 * j * HD : (2 * j + 2) * HD].rearrange(
+                        out=stats[(w, m)][:, first : first + 2, :].rearrange("p a s -> p (a s)"),
+                        in_=acc[(w, m, h)][:, 2 * j * HD : (2 * j + 2) * HD].rearrange(
                             "p (a c) -> p c a", a=2
                         ),
                     )
@@ -238,38 +244,55 @@ def tile_ltransformerdecoderblock_pa_kernel(
             )
 
         sum_squares(0)
+        root_mean_square(0)
         reciprocal(0)
         sum_squares(1)
-        reciprocal(1)
+        root_mean_square(1)
         scale_transpose(0)
+        reciprocal(1)
+        regroup_vector(0, 0, N_TILE)
+        regroup_vector(0, 1, N_TILE)
+        quantise_unit(0, 0)
         for m in range(TOKEN_TILES):
-            if m < UNITS:
-                regroup(0, m, N_TILE)
             if m + 2 < TOKEN_TILES:
                 sum_squares(m + 2)
+                root_mean_square(m + 2)
             if m + 1 < TOKEN_TILES:
                 scale_transpose(m + 1)
-            apply_gain(m)
+            if m + 2 < UNITS:
+                regroup_vector(0, m + 2, N_TILE)
             if m + 2 < TOKEN_TILES:
                 reciprocal(m + 2)
-            if m < UNITS:
-                quantise_unit(0, m)
+            apply_gain(m)
+            if m + 1 < UNITS:
+                quantise_unit(0, m + 1)
             quantise_tokens(m)
 
         steps = [(w, m) for w in range(len(weights)) for m in range(TOKEN_TILES)]
+        for j in range(SCALAR_AHEAD):
+            regroup_scalar(later_units[j][0], later_units[j][1], VECTOR_COLS)
+        for j in range(VECTOR_AHEAD):
+            regroup_vector(later_units[j][0], later_units[j][1], VECTOR_COLS)
         matmuls(0, 0)
-        for i, (w, m) in enumerate(steps):
-            prepare = w + 1 < len(weights) and m < UNITS
+        for j in range(VECTOR_AHEAD):
+            quantise_unit(later_units[j][0], later_units[j][1])
+        for i in range(len(steps) + 2):
             if i + 1 < len(steps):
                 matmuls(steps[i + 1][0], steps[i + 1][1])
-            if i > 0:
+            if i < len(steps):
+                copy_out(steps[i][0], steps[i][1])
+            if i + SCALAR_AHEAD < len(later_units):
+                w, u = later_units[i + SCALAR_AHEAD]
+                regroup_scalar(w, u, VECTOR_COLS)
+            if i + VECTOR_AHEAD < len(later_units):
+                w, u = later_units[i + VECTOR_AHEAD]
+                regroup_vector(w, u, VECTOR_COLS)
+            if 1 <= i <= len(steps):
+                head_stats(steps[i - 1][0], steps[i - 1][1])
+            if i + VECTOR_AHEAD < len(later_units):
+                w, u = later_units[i + VECTOR_AHEAD]
+                quantise_unit(w, u)
+            if 1 <= i <= len(steps):
                 sum_heads(steps[i - 1][0], steps[i - 1][1])
-            if prepare:
-                regroup(w + 1, m, VECTOR_COLS)
-            evacuate(w, m)
-            if i > 0:
-                lift_and_store(steps[i - 1][0], steps[i - 1][1])
-            if prepare:
-                quantise_unit(w + 1, m)
-        sum_heads(steps[-1][0], steps[-1][1])
-        lift_and_store(steps[-1][0], steps[-1][1])
+            if i >= 2:
+                lift_and_store(steps[i - 2][0], steps[i - 2][1])

@@ -26,11 +26,10 @@ TOKEN_TILES = TOKENS // P
 N_TILE = 512
 HALVES = E // N_TILE
 HEADS_PER_BANK = N_TILE // HD
-UNITS = PASSES * HALVES
 RUN = 4
-VECTOR_COLS = 192
-SCALAR_AHEAD = 2
-VECTOR_AHEAD = 1
+
+UNITS = PASSES * HALVES
+VECTOR_COLS = 64
 
 FLOPS = 2 * TOKENS * D * 3 * E
 
@@ -64,32 +63,35 @@ def tile_ltransformerdecoderblock_pa_kernel(
             out=gain[:], in_=ln1_w.rearrange("(g p t) -> p g t", g=PASSES, t=PACK)
         )
 
-        x_sb = {}
-        raw = {}
+        x_sb = []
+        raw = []
 
         def load_tokens(m):
-            x_sb[m] = consts.tile([P, D], BF16, name="x%d" % m)
-            nc.sync.dma_start(out=x_sb[m][:], in_=x_rows[m * P : (m + 1) * P, :])
+            x_tile = consts.tile([P, D], BF16, name="x%d" % m)
+            nc.sync.dma_start(out=x_tile[:], in_=x_rows[m * P : (m + 1) * P, :])
+            x_sb.append(x_tile)
 
-        def load_unit(w, u):
-            g, h = divmod(u, HALVES)
-            raw[(w, u)] = consts.tile([P, PACK, N_TILE], BF16, name="raw%d_%d" % (w, u))
+        def load_chunk(w, g):
+            raw_tile = consts.tile([P, PACK, E], BF16, name="raw%d_%d" % (w, g))
             nc.sync.dma_start(
-                out=raw[(w, u)][:],
-                in_=weights[w][
-                    g * K_PASS : (g + 1) * K_PASS, h * N_TILE : (h + 1) * N_TILE
-                ].rearrange("(p j) n -> p j n", j=PACK),
+                out=raw_tile[:],
+                in_=weights[w][g * K_PASS : (g + 1) * K_PASS, :].rearrange(
+                    "(p j) n -> p j n", j=PACK
+                ),
             )
+            raw.append(raw_tile)
 
-        for m in range(TOKEN_TILES):
+        load_tokens(0)
+        load_tokens(1)
+        load_chunk(0, 0)
+        for m in range(2, TOKEN_TILES):
             load_tokens(m)
-            if m < UNITS:
-                load_unit(0, m)
-        later_units = [(w, u) for w in range(1, len(weights)) for u in range(UNITS)]
-        for w, u in later_units:
-            load_unit(w, u)
+        load_chunk(0, 1)
+        for w in range(1, len(weights)):
+            for g in range(PASSES):
+                load_chunk(w, g)
 
-        sumsq = {}
+        rms = {}
         rstd = {}
         xt = {}
         xg = {}
@@ -98,17 +100,13 @@ def tile_ltransformerdecoderblock_pa_kernel(
 
         def sum_squares(m):
             squares = xwork.tile([P, D], BF16)
-            sumsq[m] = consts.tile([P, 1], F32, name="sumsq%d" % m)
+            sumsq = consts.tile([P, 1], F32, name="sumsq%d" % m)
             nc.scalar.activation(
-                out=squares[:], in_=x_sb[m][:], func=ACT.Square, accum_out=sumsq[m][:]
+                out=squares[:], in_=x_sb[m][:], func=ACT.Square, accum_out=sumsq[:]
             )
-
-        rms = {}
-
-        def root_mean_square(m):
             rms[m] = consts.tile([P, 1], F32, name="rms%d" % m)
             nc.scalar.activation(
-                out=rms[m][:], in_=sumsq[m][:], func=ACT.Sqrt, scale=1.0 / D, bias=EPS
+                out=rms[m][:], in_=sumsq[:], func=ACT.Sqrt, scale=1.0 / D, bias=EPS
             )
 
         def reciprocal(m):
@@ -151,20 +149,17 @@ def tile_ltransformerdecoderblock_pa_kernel(
         w_codes = {}
         w_scales = {}
 
-        def regroup_views(w, u):
-            if (w, u) not in wg:
-                wg[(w, u)] = wwork.tile([P, N_TILE, PACK], BF16, align_bytes=64, name="wg")
+        def regroup(w, u, vector_cols):
+            g, h = divmod(u, HALVES)
+            wg[(w, u)] = wwork.tile([P, N_TILE, PACK], BF16, align_bytes=64, name="wg")
             dst = wg[(w, u)][:].rearrange("p (c i) t -> p c t i", i=RUN)
-            src = raw[(w, u)][:].rearrange("p t (c i) -> p c t i", i=RUN)
-            return dst, src
-
-        def regroup_vector(w, u, cols):
-            dst, src = regroup_views(w, u)
-            nc.vector.tensor_copy(out=dst[:, : cols // RUN], in_=src[:, : cols // RUN])
-
-        def regroup_scalar(w, u, cols):
-            dst, src = regroup_views(w, u)
-            nc.scalar.copy(out=dst[:, cols // RUN :], in_=src[:, cols // RUN :])
+            src = raw[w * PASSES + g][:, :, h * N_TILE : (h + 1) * N_TILE].rearrange(
+                "p t (c i) -> p c t i", i=RUN
+            )
+            split = vector_cols // RUN
+            nc.vector.tensor_copy(out=dst[:, :split], in_=src[:, :split])
+            if vector_cols < N_TILE:
+                nc.scalar.copy(out=dst[:, split:], in_=src[:, split:])
 
         def quantise_unit(w, u):
             w_codes[(w, u)] = consts.tile(
@@ -198,23 +193,22 @@ def tile_ltransformerdecoderblock_pa_kernel(
                         stop=(g == PASSES - 1),
                     )
 
-        def copy_out(w, m):
+        def evacuate(w, m):
             o_sb[(w, m)] = opool.tile([P, H, HD + 1], F32, name="o_sb")
+            stats[(w, m)] = opool.tile([P, H, 3], F32, name="stats")
             for h in range(HALVES):
+                bank = acc[(w, m, h)]
                 first = h * HEADS_PER_BANK
                 nc.scalar.copy(
                     out=o_sb[(w, m)][:, first : first + HEADS_PER_BANK, 1:],
-                    in_=acc[(w, m, h)][:].rearrange("p (a c) -> p a c", c=HD),
+                    in_=bank[:].rearrange("p (a c) -> p a c", c=HD),
                 )
-
-        def head_stats(w, m):
-            stats[(w, m)] = opool.tile([P, H, 3], F32, name="stats")
-            for h in range(HALVES):
                 for j in range(HEADS_PER_BANK // 2):
-                    first = h * HEADS_PER_BANK + 2 * j
                     nc.vector.bn_stats(
-                        out=stats[(w, m)][:, first : first + 2, :].rearrange("p a s -> p (a s)"),
-                        in_=acc[(w, m, h)][:, 2 * j * HD : (2 * j + 2) * HD].rearrange(
+                        out=stats[(w, m)][:, first + 2 * j : first + 2 * j + 2, :].rearrange(
+                            "p a s -> p (a s)"
+                        ),
+                        in_=bank[:, 2 * j * HD : (2 * j + 2) * HD].rearrange(
                             "p (a c) -> p c a", a=2
                         ),
                     )
@@ -244,55 +238,38 @@ def tile_ltransformerdecoderblock_pa_kernel(
             )
 
         sum_squares(0)
-        root_mean_square(0)
         reciprocal(0)
         sum_squares(1)
-        root_mean_square(1)
-        scale_transpose(0)
         reciprocal(1)
-        regroup_vector(0, 0, N_TILE)
-        regroup_vector(0, 1, N_TILE)
-        quantise_unit(0, 0)
+        scale_transpose(0)
         for m in range(TOKEN_TILES):
+            if m < UNITS:
+                regroup(0, m, N_TILE)
             if m + 2 < TOKEN_TILES:
                 sum_squares(m + 2)
-                root_mean_square(m + 2)
             if m + 1 < TOKEN_TILES:
                 scale_transpose(m + 1)
-            if m + 2 < UNITS:
-                regroup_vector(0, m + 2, N_TILE)
+            apply_gain(m)
             if m + 2 < TOKEN_TILES:
                 reciprocal(m + 2)
-            apply_gain(m)
-            if m + 1 < UNITS:
-                quantise_unit(0, m + 1)
+            if m < UNITS:
+                quantise_unit(0, m)
             quantise_tokens(m)
 
         steps = [(w, m) for w in range(len(weights)) for m in range(TOKEN_TILES)]
-        for j in range(SCALAR_AHEAD):
-            regroup_scalar(later_units[j][0], later_units[j][1], VECTOR_COLS)
-        for j in range(VECTOR_AHEAD):
-            regroup_vector(later_units[j][0], later_units[j][1], VECTOR_COLS)
         matmuls(0, 0)
-        for j in range(VECTOR_AHEAD):
-            quantise_unit(later_units[j][0], later_units[j][1])
-        for i in range(len(steps) + 2):
+        for i, (w, m) in enumerate(steps):
+            prepare = w + 1 < len(weights) and m < UNITS
             if i + 1 < len(steps):
                 matmuls(steps[i + 1][0], steps[i + 1][1])
-            if i < len(steps):
-                copy_out(steps[i][0], steps[i][1])
-            if i + SCALAR_AHEAD < len(later_units):
-                w, u = later_units[i + SCALAR_AHEAD]
-                regroup_scalar(w, u, VECTOR_COLS)
-            if i + VECTOR_AHEAD < len(later_units):
-                w, u = later_units[i + VECTOR_AHEAD]
-                regroup_vector(w, u, VECTOR_COLS)
-            if 1 <= i <= len(steps):
-                head_stats(steps[i - 1][0], steps[i - 1][1])
-            if i + VECTOR_AHEAD < len(later_units):
-                w, u = later_units[i + VECTOR_AHEAD]
-                quantise_unit(w, u)
-            if 1 <= i <= len(steps):
+            if i > 0:
                 sum_heads(steps[i - 1][0], steps[i - 1][1])
-            if i >= 2:
-                lift_and_store(steps[i - 2][0], steps[i - 2][1])
+            if prepare:
+                regroup(w + 1, m, VECTOR_COLS)
+            evacuate(w, m)
+            if i > 0:
+                lift_and_store(steps[i - 1][0], steps[i - 1][1])
+            if prepare:
+                quantise_unit(w + 1, m)
+        sum_heads(steps[-1][0], steps[-1][1])
+        lift_and_store(steps[-1][0], steps[-1][1])

@@ -29,7 +29,7 @@ HEADS_PER_BANK = N_TILE // HD
 RUN = 4
 
 UNITS = PASSES * HALVES
-VECTOR_COLS = 64
+VECTOR_COLS = 192
 
 FLOPS = 2 * TOKENS * D * 3 * E
 
@@ -91,6 +91,7 @@ def tile_ltransformerdecoderblock_pa_kernel(
             for g in range(PASSES):
                 load_chunk(w, g)
 
+        sumsq = {}
         rms = {}
         rstd = {}
         xt = {}
@@ -100,13 +101,15 @@ def tile_ltransformerdecoderblock_pa_kernel(
 
         def sum_squares(m):
             squares = xwork.tile([P, D], BF16)
-            sumsq = consts.tile([P, 1], F32, name="sumsq%d" % m)
+            sumsq[m] = consts.tile([P, 1], F32, name="sumsq%d" % m)
             nc.scalar.activation(
-                out=squares[:], in_=x_sb[m][:], func=ACT.Square, accum_out=sumsq[:]
+                out=squares[:], in_=x_sb[m][:], func=ACT.Square, accum_out=sumsq[m][:]
             )
+
+        def root_mean_square(m):
             rms[m] = consts.tile([P, 1], F32, name="rms%d" % m)
             nc.scalar.activation(
-                out=rms[m][:], in_=sumsq[:], func=ACT.Sqrt, scale=1.0 / D, bias=EPS
+                out=rms[m][:], in_=sumsq[m][:], func=ACT.Sqrt, scale=1.0 / D, bias=EPS
             )
 
         def reciprocal(m):
@@ -178,6 +181,7 @@ def tile_ltransformerdecoderblock_pa_kernel(
         o_sb = {}
         stats = {}
         head_sumsq = {}
+        mean_sq = {}
 
         def matmuls(w, m):
             for h in range(HALVES):
@@ -193,35 +197,41 @@ def tile_ltransformerdecoderblock_pa_kernel(
                         stop=(g == PASSES - 1),
                     )
 
-        def evacuate(w, m):
-            o_sb[(w, m)] = opool.tile([P, H, HD + 1], F32, name="o_sb")
-            stats[(w, m)] = opool.tile([P, H, 3], F32, name="stats")
-            for h in range(HALVES):
-                bank = acc[(w, m, h)]
-                first = h * HEADS_PER_BANK
-                nc.scalar.copy(
-                    out=o_sb[(w, m)][:, first : first + HEADS_PER_BANK, 1:],
-                    in_=bank[:].rearrange("p (a c) -> p a c", c=HD),
+        def copy_out(w, m, h):
+            if h == 0:
+                o_sb[(w, m)] = opool.tile([P, H, HD + 1], F32, name="o_sb")
+            first = h * HEADS_PER_BANK
+            nc.scalar.copy(
+                out=o_sb[(w, m)][:, first : first + HEADS_PER_BANK, 1:],
+                in_=acc[(w, m, h)][:].rearrange("p (a c) -> p a c", c=HD),
+            )
+
+        def head_stats(w, m, h):
+            if h == 0:
+                stats[(w, m)] = opool.tile([P, H, 3], F32, name="stats")
+            for j in range(HEADS_PER_BANK // 2):
+                first = h * HEADS_PER_BANK + 2 * j
+                nc.vector.bn_stats(
+                    out=stats[(w, m)][:, first : first + 2, :].rearrange("p a s -> p (a s)"),
+                    in_=acc[(w, m, h)][:, 2 * j * HD : (2 * j + 2) * HD].rearrange(
+                        "p (a c) -> p c a", a=2
+                    ),
                 )
-                for j in range(HEADS_PER_BANK // 2):
-                    nc.vector.bn_stats(
-                        out=stats[(w, m)][:, first + 2 * j : first + 2 * j + 2, :].rearrange(
-                            "p a s -> p (a s)"
-                        ),
-                        in_=bank[:, 2 * j * HD : (2 * j + 2) * HD].rearrange(
-                            "p (a c) -> p c a", a=2
-                        ),
-                    )
+
+        def square_means(w, m):
+            mean_sq[(w, m)] = opool.tile([P, H], F32, name="mean_sq")
+            nc.vector.tensor_tensor(
+                out=mean_sq[(w, m)][:],
+                in0=stats[(w, m)][:, :, 1],
+                in1=stats[(w, m)][:, :, 1],
+                op=ALU.mult,
+            )
 
         def sum_heads(w, m):
-            mean_sq = opool.tile([P, H], F32)
-            nc.vector.tensor_tensor(
-                out=mean_sq[:], in0=stats[(w, m)][:, :, 1], in1=stats[(w, m)][:, :, 1], op=ALU.mult
-            )
             head_sumsq[(w, m)] = opool.tile([P, H], F32, name="head_sumsq")
             nc.vector.scalar_tensor_tensor(
                 out=head_sumsq[(w, m)][:],
-                in0=mean_sq[:],
+                in0=mean_sq[(w, m)][:],
                 scalar=float(HD),
                 in1=stats[(w, m)][:, :, 2],
                 op0=ALU.mult,
@@ -238,10 +248,12 @@ def tile_ltransformerdecoderblock_pa_kernel(
             )
 
         sum_squares(0)
+        root_mean_square(0)
         reciprocal(0)
         sum_squares(1)
-        reciprocal(1)
         scale_transpose(0)
+        root_mean_square(1)
+        reciprocal(1)
         for m in range(TOKEN_TILES):
             if m < UNITS:
                 regroup(0, m, N_TILE)
@@ -249,6 +261,8 @@ def tile_ltransformerdecoderblock_pa_kernel(
                 sum_squares(m + 2)
             if m + 1 < TOKEN_TILES:
                 scale_transpose(m + 1)
+            if m + 2 < TOKEN_TILES:
+                root_mean_square(m + 2)
             apply_gain(m)
             if m + 2 < TOKEN_TILES:
                 reciprocal(m + 2)
@@ -258,18 +272,24 @@ def tile_ltransformerdecoderblock_pa_kernel(
 
         steps = [(w, m) for w in range(len(weights)) for m in range(TOKEN_TILES)]
         matmuls(0, 0)
-        for i, (w, m) in enumerate(steps):
-            prepare = w + 1 < len(weights) and m < UNITS
+        for i in range(len(steps) + 2):
+            w, m = steps[min(i, len(steps) - 1)]
+            prepare = i < len(steps) and w + 1 < len(weights) and m < UNITS
             if i + 1 < len(steps):
                 matmuls(steps[i + 1][0], steps[i + 1][1])
-            if i > 0:
-                sum_heads(steps[i - 1][0], steps[i - 1][1])
             if prepare:
                 regroup(w + 1, m, VECTOR_COLS)
-            evacuate(w, m)
-            if i > 0:
-                lift_and_store(steps[i - 1][0], steps[i - 1][1])
+            if i < len(steps):
+                copy_out(w, m, 0)
+                head_stats(w, m, 0)
+            if 1 <= i <= len(steps):
+                square_means(steps[i - 1][0], steps[i - 1][1])
+            if i < len(steps):
+                copy_out(w, m, 1)
+                head_stats(w, m, 1)
+            if 1 <= i <= len(steps):
+                sum_heads(steps[i - 1][0], steps[i - 1][1])
+            if i >= 2:
+                lift_and_store(steps[i - 2][0], steps[i - 2][1])
             if prepare:
                 quantise_unit(w + 1, m)
-        sum_heads(steps[-1][0], steps[-1][1])
-        lift_and_store(steps[-1][0], steps[-1][1])

@@ -44,11 +44,10 @@ def tile_ltransformerdecoderblock_pa_kernel(
 
     with ExitStack() as ctx:
         consts = ctx.enter_context(tc.tile_pool(name="consts", bufs=1))
-        xwork = ctx.enter_context(tc.tile_pool(name="xwork", bufs=2))
-        wwork = ctx.enter_context(tc.tile_pool(name="wwork", bufs=4))
-        opool = ctx.enter_context(tc.tile_pool(name="opool", bufs=6))
+        xwork = ctx.enter_context(tc.tile_pool(name="xwork", bufs=3))
+        wwork = ctx.enter_context(tc.tile_pool(name="wwork", bufs=6))
+        opool = ctx.enter_context(tc.tile_pool(name="opool", bufs=8))
         psum = ctx.enter_context(tc.psum_pool(name="psum", bufs=8))
-        ctx.enter_context(tc.manual_schedule())
 
         one = consts.tile([P, 1], F32)
         nc.vector.memset(one[:], 1.0)

@@ -29,7 +29,7 @@ HEADS_PER_BANK = N_TILE // HD
 RUN = 4
 
 UNITS = PASSES * HALVES
-VECTOR_COLS = 192
+GPSIMD_COLS = 256
 
 FLOPS = 2 * TOKENS * D * 3 * E
 
@@ -45,7 +45,8 @@ def tile_ltransformerdecoderblock_pa_kernel(
     with ExitStack() as ctx:
         consts = ctx.enter_context(tc.tile_pool(name="consts", bufs=1))
         xwork = ctx.enter_context(tc.tile_pool(name="xwork", bufs=3))
-        wwork = ctx.enter_context(tc.tile_pool(name="wwork", bufs=6))
+        wwork = ctx.enter_context(tc.tile_pool(name="wwork", bufs=4))
+        gwork = ctx.enter_context(tc.tile_pool(name="gwork", bufs=1))
         opool = ctx.enter_context(tc.tile_pool(name="opool", bufs=8))
         psum = ctx.enter_context(tc.psum_pool(name="psum", bufs=8))
 
@@ -54,13 +55,26 @@ def tile_ltransformerdecoderblock_pa_kernel(
         warm = consts.tile([P, 1], F32)
         nc.scalar.activation(out=warm[:], in_=one[:], func=ACT.Sqrt)
 
+        gain_row = consts.tile([P, D], BF16)
+        nc.vector.memset(gain_row[:], 0.0)
+        nc.sync.dma_start(out=gain_row[0:1, :], in_=ln1_w.rearrange("(o d) -> o d", o=1))
+        ones = consts.tile([P, P], BF16)
+        nc.vector.memset(ones[:], 1.0)
+
         ident = consts.tile([P, P], F32)
         make_identity(nc, ident[:])
 
-        gain = consts.tile([P, PASSES, PACK], BF16)
-        nc.scalar.dma_start(
-            out=gain[:], in_=ln1_w.rearrange("(g p t) -> p g t", g=PASSES, t=PACK)
-        )
+        gain_all = []
+        for h in range(D // N_TILE):
+            spread = psum.tile([P, N_TILE], F32, tag="bank", name="spread")
+            nc.tensor.matmul(
+                out=spread[:],
+                lhsT=ones[:],
+                rhs=gain_row[:, h * N_TILE : (h + 1) * N_TILE],
+                start=True,
+                stop=True,
+            )
+            gain_all.append(spread)
 
         x_sb = []
         raw = []
@@ -116,27 +130,36 @@ def tile_ltransformerdecoderblock_pa_kernel(
             nc.vector.reciprocal(out=rstd[m][:], in_=rms[m][:])
 
         def scale_transpose(m):
-            xs = xwork.tile([P, PASSES, PACK, P], F32)
-            nc.scalar.activation(
-                out=xs[:],
-                in_=x_sb[m][:].rearrange("p (g c t) -> p g t c", g=PASSES, t=PACK),
-                func=ACT.Copy,
-                scale=rstd[m][:],
-            )
+            normed = xwork.tile([P, D], BF16)
+            for h in range(D // N_TILE):
+                cols = slice(h * N_TILE, (h + 1) * N_TILE)
+                nc.vector.scalar_tensor_tensor(
+                    out=normed[:, cols],
+                    in0=x_sb[m][:, cols],
+                    scalar=rstd[m][:],
+                    in1=gain_all[h][:],
+                    op0=ALU.mult,
+                    op1=ALU.mult,
+                )
+            words = normed[:].bitcast(F32)
+            xt[m] = psum.tile([P, PASSES, 2, P], F32, tag="bank", name="xt")
             for g in range(PASSES):
-                xt[(m, g)] = psum.tile([P, PACK, P], F32, tag="bank", name="xt")
-                for t in range(PACK):
-                    nc.tensor.transpose(xt[(m, g)][:, t, :], xs[:, g, t, :], ident[:])
+                for u in range(2):
+                    nc.tensor.transpose(
+                        xt[m][:, g, u, :],
+                        words[:, g * 2 * P + u : (g + 1) * 2 * P : 2],
+                        ident[:],
+                    )
 
         def apply_gain(m):
             xg[m] = xwork.tile([P, PASSES, P, PACK], BF16, align_bytes=64, name="xg")
-            for g in range(PASSES):
-                nc.vector.tensor_tensor(
-                    out=xg[m][:, g, :, :],
-                    in0=xt[(m, g)][:].rearrange("p t r -> p r t"),
-                    in1=gain[:, g, :].unsqueeze(1).to_broadcast([P, P, PACK]),
-                    op=ALU.mult,
-                )
+            nc.scalar.copy(
+                out=xg[m][:]
+                .rearrange("p g r t -> p (g r t)")
+                .bitcast(F32)
+                .rearrange("p (g r u) -> p g r u", g=PASSES, u=2),
+                in_=xt[m][:].rearrange("p g u r -> p g r u"),
+            )
 
         def quantise_tokens(m):
             x_codes[m] = consts.tile([P, PASSES * P], U32, name="xc%d" % m, align_bytes=64)
@@ -148,20 +171,43 @@ def tile_ltransformerdecoderblock_pa_kernel(
             )
 
         wg = {}
+        wg_g = {}
+        wg_s = {}
         w_codes = {}
         w_scales = {}
 
-        def regroup(w, u, vector_cols):
+        def regroup(w, u):
             g, h = divmod(u, HALVES)
             wg[(w, u)] = wwork.tile([P, N_TILE, PACK], BF16, align_bytes=64, name="wg")
             dst = wg[(w, u)][:].rearrange("p (c i) t -> p c t i", i=RUN)
             src = raw[w * PASSES + g][:, :, h * N_TILE : (h + 1) * N_TILE].rearrange(
                 "p t (c i) -> p c t i", i=RUN
             )
-            split = vector_cols // RUN
-            nc.vector.tensor_copy(out=dst[:, :split], in_=src[:, :split])
-            if vector_cols < N_TILE:
-                nc.scalar.copy(out=dst[:, split:], in_=src[:, split:])
+            nc.vector.tensor_copy(out=dst, in_=src)
+
+        def regroup_shared(w, u):
+            g, h = divmod(u, HALVES)
+            first = h * N_TILE
+            wg_g[(w, u)] = gwork.tile([P, GPSIMD_COLS, PACK], BF16, align_bytes=64, name="wg_g")
+            nc.gpsimd.tensor_scalar(
+                out=wg_g[(w, u)][:],
+                in0=raw[w * PASSES + g][:, :, first : first + GPSIMD_COLS].rearrange(
+                    "p t c -> p c t"
+                ),
+                scalar1=1.0,
+                scalar2=0.0,
+                op0=ALU.mult,
+                op1=ALU.add,
+            )
+            wg_s[(w, u)] = wwork.tile(
+                [P, N_TILE - GPSIMD_COLS, PACK], BF16, align_bytes=64, name="wg_s"
+            )
+            nc.scalar.copy(
+                out=wg_s[(w, u)][:].rearrange("p (c i) t -> p c t i", i=RUN),
+                in_=raw[w * PASSES + g][:, :, first + GPSIMD_COLS : first + N_TILE].rearrange(
+                    "p t (c i) -> p c t i", i=RUN
+                ),
+            )
 
         def quantise_unit(w, u):
             w_codes[(w, u)] = consts.tile(
@@ -170,11 +216,19 @@ def tile_ltransformerdecoderblock_pa_kernel(
             w_scales[(w, u)] = consts.tile(
                 [P, N_TILE], U8, name="wsc%d_%d" % (w, u), align_bytes=64
             )
-            nc.vector.quantize_mx(
-                out=w_codes[(w, u)][:].bitcast(FP8X4),
-                scales=w_scales[(w, u)][:],
-                in_=wg[(w, u)][:].rearrange("p n t -> p (n t)"),
-            )
+            if w == 0:
+                pieces = [(wg[(w, u)], 0, N_TILE)]
+            else:
+                pieces = [
+                    (wg_g[(w, u)], 0, GPSIMD_COLS),
+                    (wg_s[(w, u)], GPSIMD_COLS, N_TILE),
+                ]
+            for grouped, lo, hi in pieces:
+                nc.vector.quantize_mx(
+                    out=w_codes[(w, u)][:, lo:hi].bitcast(FP8X4),
+                    scales=w_scales[(w, u)][:, lo:hi],
+                    in_=grouped[:].rearrange("p n t -> p (n t)"),
+                )
 
         acc = {}
         o_sb = {}
@@ -255,7 +309,7 @@ def tile_ltransformerdecoderblock_pa_kernel(
         reciprocal(1)
         for m in range(TOKEN_TILES):
             if m < UNITS:
-                regroup(0, m, N_TILE)
+                regroup(0, m)
             if m + 2 < TOKEN_TILES:
                 sum_squares(m + 2)
             if m + 1 < TOKEN_TILES:
@@ -277,7 +331,7 @@ def tile_ltransformerdecoderblock_pa_kernel(
             if i + 1 < len(steps):
                 matmuls(steps[i + 1][0], steps[i + 1][1])
             if prepare:
-                regroup(w + 1, m, VECTOR_COLS)
+                regroup_shared(w + 1, m)
             if i < len(steps):
                 copy_out(w, m, 0)
                 head_stats(w, m, 0)

@@ -27,9 +27,7 @@ N_TILE = 512
 HALVES = E // N_TILE
 HEADS_PER_BANK = N_TILE // HD
 RUN = 4
-
-UNITS = PASSES * HALVES
-GPSIMD_COLS = 256
+AHEAD = 2
 
 FLOPS = 2 * TOKENS * D * 3 * E
 
@@ -45,10 +43,10 @@ def tile_ltransformerdecoderblock_pa_kernel(
     with ExitStack() as ctx:
         consts = ctx.enter_context(tc.tile_pool(name="consts", bufs=1))
         xwork = ctx.enter_context(tc.tile_pool(name="xwork", bufs=3))
-        wwork = ctx.enter_context(tc.tile_pool(name="wwork", bufs=4))
-        gwork = ctx.enter_context(tc.tile_pool(name="gwork", bufs=1))
+        wwork = ctx.enter_context(tc.tile_pool(name="wwork", bufs=2))
         opool = ctx.enter_context(tc.tile_pool(name="opool", bufs=8))
         psum = ctx.enter_context(tc.psum_pool(name="psum", bufs=8))
+        ctx.enter_context(tc.manual_schedule())
 
         one = consts.tile([P, 1], F32)
         nc.vector.memset(one[:], 1.0)
@@ -56,25 +54,19 @@ def tile_ltransformerdecoderblock_pa_kernel(
         nc.scalar.activation(out=warm[:], in_=one[:], func=ACT.Sqrt)
 
         gain_row = consts.tile([P, D], BF16)
-        nc.vector.memset(gain_row[:], 0.0)
-        nc.sync.dma_start(out=gain_row[0:1, :], in_=ln1_w.rearrange("(o d) -> o d", o=1))
+        nc.gpsimd.memset(gain_row[:].bitcast(F32), 0.0)
         ones = consts.tile([P, P], BF16)
         nc.vector.memset(ones[:], 1.0)
 
         ident = consts.tile([P, P], F32)
         make_identity(nc, ident[:])
 
-        gain_all = []
-        for h in range(D // N_TILE):
-            spread = psum.tile([P, N_TILE], F32, tag="bank", name="spread")
-            nc.tensor.matmul(
-                out=spread[:],
-                lhsT=ones[:],
-                rhs=gain_row[:, h * N_TILE : (h + 1) * N_TILE],
-                start=True,
-                stop=True,
-            )
-            gain_all.append(spread)
+        token = consts.tile([P, 1], F32)
+
+        def open_gate():
+            nc.vector.memset(token[:], 1.0)
+
+        open_gate()
 
         x_sb = []
         raw = []
@@ -95,6 +87,7 @@ def tile_ltransformerdecoderblock_pa_kernel(
             raw.append(raw_tile)
 
         load_tokens(0)
+        nc.sync.dma_start(out=gain_row[0:1, :], in_=ln1_w.rearrange("(o d) -> o d", o=1))
         load_tokens(1)
         load_chunk(0, 0)
         for m in range(2, TOKEN_TILES):
@@ -104,7 +97,18 @@ def tile_ltransformerdecoderblock_pa_kernel(
             for g in range(PASSES):
                 load_chunk(w, g)
 
-        sumsq = {}
+        gain_all = []
+        for h in range(D // N_TILE):
+            spread = psum.tile([P, N_TILE], F32, tag="bank", name="spread")
+            nc.tensor.matmul(
+                out=spread[:],
+                lhsT=ones[:],
+                rhs=gain_row[:, h * N_TILE : (h + 1) * N_TILE],
+                start=True,
+                stop=True,
+            )
+            gain_all.append(spread)
+
         rms = {}
         rstd = {}
         xt = {}
@@ -112,24 +116,22 @@ def tile_ltransformerdecoderblock_pa_kernel(
         x_codes = {}
         x_scales = {}
 
-        def sum_squares(m):
-            squares = xwork.tile([P, D], BF16)
-            sumsq[m] = consts.tile([P, 1], F32, name="sumsq%d" % m)
-            nc.scalar.activation(
-                out=squares[:], in_=x_sb[m][:], func=ACT.Square, accum_out=sumsq[m][:]
-            )
-
         def root_mean_square(m):
+            squares = xwork.tile([P, D], BF16)
+            sumsq = consts.tile([P, 1], F32, name="sumsq%d" % m)
+            nc.scalar.activation(
+                out=squares[:], in_=x_sb[m][:], func=ACT.Square, accum_out=sumsq[:]
+            )
             rms[m] = consts.tile([P, 1], F32, name="rms%d" % m)
             nc.scalar.activation(
-                out=rms[m][:], in_=sumsq[m][:], func=ACT.Sqrt, scale=1.0 / D, bias=EPS
+                out=rms[m][:], in_=sumsq[:], func=ACT.Sqrt, scale=1.0 / D, bias=EPS
             )
 
         def reciprocal(m):
             rstd[m] = consts.tile([P, 1], F32, name="rstd%d" % m)
             nc.vector.reciprocal(out=rstd[m][:], in_=rms[m][:])
 
-        def scale_transpose(m):
+        def norm_transpose(m):
             normed = xwork.tile([P, D], BF16)
             for h in range(D // N_TILE):
                 cols = slice(h * N_TILE, (h + 1) * N_TILE)
@@ -151,7 +153,7 @@ def tile_ltransformerdecoderblock_pa_kernel(
                         ident[:],
                     )
 
-        def apply_gain(m):
+        def copy_tokens(m):
             xg[m] = xwork.tile([P, PASSES, P, PACK], BF16, align_bytes=64, name="xg")
             nc.scalar.copy(
                 out=xg[m][:]
@@ -171,43 +173,32 @@ def tile_ltransformerdecoderblock_pa_kernel(
             )
 
         wg = {}
-        wg_g = {}
-        wg_s = {}
         w_codes = {}
         w_scales = {}
+        quantised = set()
 
-        def regroup(w, u):
+        def regroup(engine, w, u):
             g, h = divmod(u, HALVES)
-            wg[(w, u)] = wwork.tile([P, N_TILE, PACK], BF16, align_bytes=64, name="wg")
+            source = raw[w * PASSES + g][:, :, h * N_TILE : (h + 1) * N_TILE]
+            if engine == "gpsimd":
+                wg[(w, u)] = wwork.tile([P, N_TILE, PACK], BF16, align_bytes=64, name="wg_g")
+                nc.gpsimd.tensor_scalar(
+                    out=wg[(w, u)][:],
+                    in0=source.rearrange("p t c -> p c t"),
+                    scalar1=token[:],
+                    scalar2=0.0,
+                    op0=ALU.mult,
+                    op1=ALU.add,
+                )
+                return
+            name = "wg_s" if engine == "scalar" else "wg_v"
+            wg[(w, u)] = wwork.tile([P, N_TILE, PACK], BF16, align_bytes=64, name=name)
             dst = wg[(w, u)][:].rearrange("p (c i) t -> p c t i", i=RUN)
-            src = raw[w * PASSES + g][:, :, h * N_TILE : (h + 1) * N_TILE].rearrange(
-                "p t (c i) -> p c t i", i=RUN
-            )
-            nc.vector.tensor_copy(out=dst, in_=src)
-
-        def regroup_shared(w, u):
-            g, h = divmod(u, HALVES)
-            first = h * N_TILE
-            wg_g[(w, u)] = gwork.tile([P, GPSIMD_COLS, PACK], BF16, align_bytes=64, name="wg_g")
-            nc.gpsimd.tensor_scalar(
-                out=wg_g[(w, u)][:],
-                in0=raw[w * PASSES + g][:, :, first : first + GPSIMD_COLS].rearrange(
-                    "p t c -> p c t"
-                ),
-                scalar1=1.0,
-                scalar2=0.0,
-                op0=ALU.mult,
-                op1=ALU.add,
-            )
-            wg_s[(w, u)] = wwork.tile(
-                [P, N_TILE - GPSIMD_COLS, PACK], BF16, align_bytes=64, name="wg_s"
-            )
-            nc.scalar.copy(
-                out=wg_s[(w, u)][:].rearrange("p (c i) t -> p c t i", i=RUN),
-                in_=raw[w * PASSES + g][:, :, first + GPSIMD_COLS : first + N_TILE].rearrange(
-                    "p t (c i) -> p c t i", i=RUN
-                ),
-            )
+            src = source.rearrange("p t (c i) -> p c t i", i=RUN)
+            if engine == "scalar":
+                nc.scalar.copy(out=dst, in_=src)
+            else:
+                nc.vector.tensor_copy(out=dst, in_=src)
 
         def quantise_unit(w, u):
             w_codes[(w, u)] = consts.tile(
@@ -216,133 +207,173 @@ def tile_ltransformerdecoderblock_pa_kernel(
             w_scales[(w, u)] = consts.tile(
                 [P, N_TILE], U8, name="wsc%d_%d" % (w, u), align_bytes=64
             )
-            if w == 0:
-                pieces = [(wg[(w, u)], 0, N_TILE)]
-            else:
-                pieces = [
-                    (wg_g[(w, u)], 0, GPSIMD_COLS),
-                    (wg_s[(w, u)], GPSIMD_COLS, N_TILE),
-                ]
-            for grouped, lo, hi in pieces:
-                nc.vector.quantize_mx(
-                    out=w_codes[(w, u)][:, lo:hi].bitcast(FP8X4),
-                    scales=w_scales[(w, u)][:, lo:hi],
-                    in_=grouped[:].rearrange("p n t -> p (n t)"),
-                )
+            nc.vector.quantize_mx(
+                out=w_codes[(w, u)][:].bitcast(FP8X4),
+                scales=w_scales[(w, u)][:],
+                in_=wg[(w, u)][:].rearrange("p n t -> p (n t)"),
+            )
+            quantised.add((w, u))
 
+        steps = [(w, m) for w in range(len(weights)) for m in range(TOKEN_TILES)]
+        banks = [(i, h) for i in range(len(steps)) for h in range(HALVES)]
+        issued = []
         acc = {}
         o_sb = {}
-        stats = {}
-        head_sumsq = {}
-        mean_sq = {}
 
-        def matmuls(w, m):
-            for h in range(HALVES):
-                acc[(w, m, h)] = psum.tile([P, N_TILE], F32, tag="bank", name="acc")
+        def matmuls(last_step):
+            for i, h in banks[len(issued) :]:
+                w, m = steps[i]
+                units = [g * HALVES + h for g in range(PASSES)]
+                if i > last_step or any((w, u) not in quantised for u in units):
+                    return
+                issued.append((i, h))
+                acc[(i, h)] = psum.tile([P, N_TILE], F32, tag="bank", name="acc")
                 for g in range(PASSES):
                     nc.tensor.matmul_mx(
-                        out=acc[(w, m, h)][:],
+                        out=acc[(i, h)][:],
                         lhsT=x_codes[m][:, g * P : (g + 1) * P].bitcast(FP8X4),
                         lhsT_scale=x_scales[m][:, g * P : (g + 1) * P],
-                        rhs=w_codes[(w, g * HALVES + h)][:].bitcast(FP8X4),
-                        rhs_scale=w_scales[(w, g * HALVES + h)][:],
+                        rhs=w_codes[(w, units[g])][:].bitcast(FP8X4),
+                        rhs_scale=w_scales[(w, units[g])][:],
                         start=(g == 0),
                         stop=(g == PASSES - 1),
                     )
 
-        def copy_out(w, m, h):
+        def copy_out(i, h):
             if h == 0:
-                o_sb[(w, m)] = opool.tile([P, H, HD + 1], F32, name="o_sb")
+                o_sb[i] = opool.tile([P, H, HD + 1], F32, name="o_sb")
             first = h * HEADS_PER_BANK
             nc.scalar.copy(
-                out=o_sb[(w, m)][:, first : first + HEADS_PER_BANK, 1:],
-                in_=acc[(w, m, h)][:].rearrange("p (a c) -> p a c", c=HD),
+                out=o_sb[i][:, first : first + HEADS_PER_BANK, 1:],
+                in_=acc[(i, h)][:].rearrange("p (a c) -> p a c", c=HD),
             )
 
-        def head_stats(w, m, h):
-            if h == 0:
-                stats[(w, m)] = opool.tile([P, H, 3], F32, name="stats")
+        def head_stats(stats, k, i, h):
             for j in range(HEADS_PER_BANK // 2):
                 first = h * HEADS_PER_BANK + 2 * j
                 nc.vector.bn_stats(
-                    out=stats[(w, m)][:, first : first + 2, :].rearrange("p a s -> p (a s)"),
-                    in_=acc[(w, m, h)][:, 2 * j * HD : (2 * j + 2) * HD].rearrange(
+                    out=stats[:, k, first : first + 2, :].rearrange("p a s -> p (a s)"),
+                    in_=acc[(i, h)][:, 2 * j * HD : (2 * j + 2) * HD].rearrange(
                         "p (a c) -> p c a", a=2
                     ),
                 )
 
-        def square_means(w, m):
-            mean_sq[(w, m)] = opool.tile([P, H], F32, name="mean_sq")
-            nc.vector.tensor_tensor(
-                out=mean_sq[(w, m)][:],
-                in0=stats[(w, m)][:, :, 1],
-                in1=stats[(w, m)][:, :, 1],
-                op=ALU.mult,
-            )
+        def new_stats(count):
+            return opool.tile([P, count, H, 3], F32, name="stats")
 
-        def sum_heads(w, m):
-            head_sumsq[(w, m)] = opool.tile([P, H], F32, name="head_sumsq")
+        def square_means(stats, count):
+            mean_sq = opool.tile([P, count, H], F32, name="mean_sq")
+            nc.vector.tensor_tensor(
+                out=mean_sq[:], in0=stats[:, :, :, 1], in1=stats[:, :, :, 1], op=ALU.mult
+            )
+            return mean_sq
+
+        def sum_heads(stats, mean_sq, count):
+            head_sumsq = opool.tile([P, count, H], F32, name="head_sumsq")
             nc.vector.scalar_tensor_tensor(
-                out=head_sumsq[(w, m)][:],
-                in0=mean_sq[(w, m)][:],
+                out=head_sumsq[:],
+                in0=mean_sq[:],
                 scalar=float(HD),
-                in1=stats[(w, m)][:, :, 2],
+                in1=stats[:, :, :, 2],
                 op0=ALU.mult,
                 op1=ALU.add,
             )
+            return head_sumsq
 
-        def lift_and_store(w, m):
+        def lift_and_store(head_sumsq, k, i):
+            w, m = steps[i]
             nc.scalar.activation(
-                out=o_sb[(w, m)][:, :, 0], in_=head_sumsq[(w, m)][:], func=ACT.Sqrt, bias=1.0 / CURV
+                out=o_sb[i][:, :, 0], in_=head_sumsq[:, k, :], func=ACT.Sqrt, bias=1.0 / CURV
             )
             nc.sync.dma_start(
                 out=outputs[w][m * P : (m + 1) * P, :],
-                in_=o_sb[(w, m)][:].rearrange("p h c -> p (h c)"),
+                in_=o_sb[i][:].rearrange("p h c -> p (h c)"),
             )
 
-        sum_squares(0)
         root_mean_square(0)
         reciprocal(0)
-        sum_squares(1)
-        scale_transpose(0)
         root_mean_square(1)
+        regroup("gpsimd", 0, 0)
+        norm_transpose(0)
         reciprocal(1)
-        for m in range(TOKEN_TILES):
-            if m < UNITS:
-                regroup(0, m)
-            if m + 2 < TOKEN_TILES:
-                sum_squares(m + 2)
-            if m + 1 < TOKEN_TILES:
-                scale_transpose(m + 1)
-            if m + 2 < TOKEN_TILES:
-                root_mean_square(m + 2)
-            apply_gain(m)
-            if m + 2 < TOKEN_TILES:
-                reciprocal(m + 2)
-            if m < UNITS:
-                quantise_unit(0, m)
-            quantise_tokens(m)
+        norm_transpose(1)
+        root_mean_square(2)
+        copy_tokens(0)
+        root_mean_square(3)
+        copy_tokens(1)
+        reciprocal(2)
+        norm_transpose(2)
 
-        steps = [(w, m) for w in range(len(weights)) for m in range(TOKEN_TILES)]
-        matmuls(0, 0)
-        for i in range(len(steps) + 2):
-            w, m = steps[min(i, len(steps) - 1)]
-            prepare = i < len(steps) and w + 1 < len(weights) and m < UNITS
-            if i + 1 < len(steps):
-                matmuls(steps[i + 1][0], steps[i + 1][1])
-            if prepare:
-                regroup_shared(w + 1, m)
-            if i < len(steps):
-                copy_out(w, m, 0)
-                head_stats(w, m, 0)
-            if 1 <= i <= len(steps):
-                square_means(steps[i - 1][0], steps[i - 1][1])
-            if i < len(steps):
-                copy_out(w, m, 1)
-                head_stats(w, m, 1)
-            if 1 <= i <= len(steps):
-                sum_heads(steps[i - 1][0], steps[i - 1][1])
-            if i >= 2:
-                lift_and_store(steps[i - 2][0], steps[i - 2][1])
-            if prepare:
-                quantise_unit(w + 1, m)
+        quantise_unit(0, 0)
+        quantise_tokens(0)
+        quantise_tokens(1)
+        open_gate()
+
+        regroup("gpsimd", 0, 2)
+        root_mean_square(4)
+        copy_tokens(2)
+        regroup("scalar", 0, 1)
+        reciprocal(3)
+        norm_transpose(3)
+        reciprocal(4)
+        norm_transpose(4)
+        copy_tokens(3)
+        copy_tokens(4)
+        regroup("scalar", 1, 1)
+
+        quantise_unit(0, 2)
+        matmuls(1)
+        regroup("vector", 0, 3)
+        quantise_unit(0, 1)
+        quantise_tokens(2)
+        quantise_unit(0, 3)
+        matmuls(1)
+        quantise_tokens(3)
+        quantise_tokens(4)
+        open_gate()
+
+        gpsimd_units = [(1, 0), (1, 2), (2, 0), (2, 2), (2, 1)]
+        scalar_units = {0: (1, 3), 2: (2, 3)}
+        scalar_ready = {0: (1, 1), 1: (1, 3), 3: (2, 3)}
+        to_lift = []
+        for s in range(len(gpsimd_units)):
+            regroup("gpsimd", gpsimd_units[s][0], gpsimd_units[s][1])
+            stats = new_stats(2)
+            for k in range(2):
+                i = 2 * s + k
+                matmuls(i + AHEAD)
+                for h in range(HALVES):
+                    head_stats(stats, k, i, h)
+                    copy_out(i, h)
+                if k == 0:
+                    for sums, kk, ii in to_lift:
+                        lift_and_store(sums, kk, ii)
+                    to_lift = []
+                    if s in scalar_units:
+                        regroup("scalar", scalar_units[s][0], scalar_units[s][1])
+            mean_sq = square_means(stats, 2)
+            if s in scalar_ready:
+                quantise_unit(scalar_ready[s][0], scalar_ready[s][1])
+            quantise_unit(gpsimd_units[s][0], gpsimd_units[s][1])
+            head_sumsq = sum_heads(stats, mean_sq, 2)
+            open_gate()
+            to_lift = [(head_sumsq, 0, 2 * s), (head_sumsq, 1, 2 * s + 1)]
+
+        before = None
+        for i in range(2 * len(gpsimd_units), len(steps)):
+            matmuls(i + AHEAD)
+            stats = new_stats(1)
+            head_stats(stats, 0, i, 0)
+            copy_out(i, 0)
+            if before is not None:
+                mean_sq = square_means(before[0], 1)
+            head_stats(stats, 0, i, 1)
+            copy_out(i, 1)
+            if before is not None:
+                lift_and_store(sum_heads(before[0], mean_sq, 1), 0, before[1])
+            for sums, kk, ii in to_lift:
+                lift_and_store(sums, kk, ii)
+            to_lift = []
+            before = (stats, i)
+        mean_sq = square_means(before[0], 1)
+        lift_and_store(sum_heads(before[0], mean_sq, 1), 0, before[1])

@@ -69,30 +69,44 @@ def tile_ltransformerdecoderblock_pa_kernel(
         open_gate()
 
         x_sb = []
-        raw = []
+        raw = {}
 
         def load_tokens(m):
             x_tile = consts.tile([P, D], BF16, name="x%d" % m)
             nc.sync.dma_start(out=x_tile[:], in_=x_rows[m * P : (m + 1) * P, :])
             x_sb.append(x_tile)
 
+        def load_unit(w, u):
+            g, h = divmod(u, HALVES)
+            raw[(w, u)] = consts.tile([P, PACK, N_TILE], BF16, name="raw%d_%d" % (w, u))
+            nc.sync.dma_start(
+                out=raw[(w, u)][:],
+                in_=weights[w][
+                    g * K_PASS : (g + 1) * K_PASS, h * N_TILE : (h + 1) * N_TILE
+                ].rearrange("(p j) n -> p j n", j=PACK),
+            )
+
         def load_chunk(w, g):
-            raw_tile = consts.tile([P, PACK, E], BF16, name="raw%d_%d" % (w, g))
+            raw_tile = consts.tile([P, PACK, E], BF16, name="raw%d_g%d" % (w, g))
             nc.sync.dma_start(
                 out=raw_tile[:],
                 in_=weights[w][g * K_PASS : (g + 1) * K_PASS, :].rearrange(
                     "(p j) n -> p j n", j=PACK
                 ),
             )
-            raw.append(raw_tile)
+            for h in range(HALVES):
+                raw[(w, g * HALVES + h)] = raw_tile[:, :, h * N_TILE : (h + 1) * N_TILE]
 
         load_tokens(0)
         nc.sync.dma_start(out=gain_row[0:1, :], in_=ln1_w.rearrange("(o d) -> o d", o=1))
         load_tokens(1)
-        load_chunk(0, 0)
-        for m in range(2, TOKEN_TILES):
-            load_tokens(m)
-        load_chunk(0, 1)
+        load_unit(0, 0)
+        load_tokens(2)
+        load_unit(0, 2)
+        load_tokens(3)
+        load_tokens(4)
+        load_unit(0, 1)
+        load_unit(0, 3)
         for w in range(1, len(weights)):
             for g in range(PASSES):
                 load_chunk(w, g)
@@ -131,7 +145,7 @@ def tile_ltransformerdecoderblock_pa_kernel(
             rstd[m] = consts.tile([P, 1], F32, name="rstd%d" % m)
             nc.vector.reciprocal(out=rstd[m][:], in_=rms[m][:])
 
-        def norm_transpose(m):
+        def norm_transpose(m, between=None):
             normed = xwork.tile([P, D], BF16)
             for h in range(D // N_TILE):
                 cols = slice(h * N_TILE, (h + 1) * N_TILE)
@@ -143,6 +157,8 @@ def tile_ltransformerdecoderblock_pa_kernel(
                     op0=ALU.mult,
                     op1=ALU.mult,
                 )
+                if h == 0 and between is not None:
+                    reciprocal(between)
             words = normed[:].bitcast(F32)
             xt[m] = psum.tile([P, PASSES, 2, P], F32, tag="bank", name="xt")
             for g in range(PASSES):
@@ -178,8 +194,7 @@ def tile_ltransformerdecoderblock_pa_kernel(
         quantised = set()
 
         def regroup(engine, w, u):
-            g, h = divmod(u, HALVES)
-            source = raw[w * PASSES + g][:, :, h * N_TILE : (h + 1) * N_TILE]
+            source = raw[(w, u)][:, :, :]
             if engine == "gpsimd":
                 wg[(w, u)] = wwork.tile([P, N_TILE, PACK], BF16, align_bytes=64, name="wg_g")
                 nc.gpsimd.tensor_scalar(
@@ -200,19 +215,24 @@ def tile_ltransformerdecoderblock_pa_kernel(
             else:
                 nc.vector.tensor_copy(out=dst, in_=src)
 
-        def quantise_unit(w, u):
-            w_codes[(w, u)] = consts.tile(
-                [P, N_TILE], U32, name="wc%d_%d" % (w, u), align_bytes=64
-            )
-            w_scales[(w, u)] = consts.tile(
-                [P, N_TILE], U8, name="wsc%d_%d" % (w, u), align_bytes=64
-            )
+        def quantise_columns(w, u, lo, hi):
+            if lo == 0:
+                w_codes[(w, u)] = consts.tile(
+                    [P, N_TILE], U32, name="wc%d_%d" % (w, u), align_bytes=64
+                )
+                w_scales[(w, u)] = consts.tile(
+                    [P, N_TILE], U8, name="wsc%d_%d" % (w, u), align_bytes=64
+                )
             nc.vector.quantize_mx(
-                out=w_codes[(w, u)][:].bitcast(FP8X4),
-                scales=w_scales[(w, u)][:],
-                in_=wg[(w, u)][:].rearrange("p n t -> p (n t)"),
+                out=w_codes[(w, u)][:, lo:hi].bitcast(FP8X4),
+                scales=w_scales[(w, u)][:, lo:hi],
+                in_=wg[(w, u)][:, lo:hi, :].rearrange("p n t -> p (n t)"),
             )
-            quantised.add((w, u))
+            if hi == N_TILE:
+                quantised.add((w, u))
+
+        def quantise_unit(w, u):
+            quantise_columns(w, u, 0, N_TILE)
 
         steps = [(w, m) for w in range(len(weights)) for m in range(TOKEN_TILES)]
         banks = [(i, h) for i in range(len(steps)) for h in range(HALVES)]
@@ -307,15 +327,14 @@ def tile_ltransformerdecoderblock_pa_kernel(
         quantise_unit(0, 0)
         quantise_tokens(0)
         quantise_tokens(1)
+        reciprocal(3)
         open_gate()
 
         regroup("gpsimd", 0, 2)
         root_mean_square(4)
         copy_tokens(2)
         regroup("scalar", 0, 1)
-        reciprocal(3)
-        norm_transpose(3)
-        reciprocal(4)
+        norm_transpose(3, between=4)
         norm_transpose(4)
         copy_tokens(3)
         copy_tokens(4)
@@ -351,10 +370,14 @@ def tile_ltransformerdecoderblock_pa_kernel(
                     to_lift = []
                     if s in scalar_units:
                         regroup("scalar", scalar_units[s][0], scalar_units[s][1])
-            mean_sq = square_means(stats, 2)
             if s in scalar_ready:
                 quantise_unit(scalar_ready[s][0], scalar_ready[s][1])
-            quantise_unit(gpsimd_units[s][0], gpsimd_units[s][1])
+                mean_sq = square_means(stats, 2)
+                quantise_unit(gpsimd_units[s][0], gpsimd_units[s][1])
+            else:
+                quantise_columns(gpsimd_units[s][0], gpsimd_units[s][1], 0, N_TILE // 2)
+                mean_sq = square_means(stats, 2)
+                quantise_columns(gpsimd_units[s][0], gpsimd_units[s][1], N_TILE // 2, N_TILE)
             head_sumsq = sum_heads(stats, mean_sq, 2)
             open_gate()
             to_lift = [(head_sumsq, 0, 2 * s), (head_sumsq, 1, 2 * s + 1)]

@@ -27,7 +27,9 @@ N_TILE = 512
 HALVES = E // N_TILE
 HEADS_PER_BANK = N_TILE // HD
 RUN = 4
-AHEAD = 2
+AHEAD = 3
+SLOT_BANKS = 5
+FIRST_BANKS = 3
 
 FLOPS = 2 * TOKENS * D * 3 * E
 
@@ -44,7 +46,7 @@ def tile_ltransformerdecoderblock_pa_kernel(
         consts = ctx.enter_context(tc.tile_pool(name="consts", bufs=1))
         xwork = ctx.enter_context(tc.tile_pool(name="xwork", bufs=3))
         wwork = ctx.enter_context(tc.tile_pool(name="wwork", bufs=2))
-        opool = ctx.enter_context(tc.tile_pool(name="opool", bufs=8))
+        opool = ctx.enter_context(tc.tile_pool(name="opool", bufs=1))
         psum = ctx.enter_context(tc.psum_pool(name="psum", bufs=8))
         ctx.enter_context(tc.manual_schedule())
 
@@ -170,7 +172,7 @@ def tile_ltransformerdecoderblock_pa_kernel(
                     )
 
         def copy_tokens(m):
-            xg[m] = xwork.tile([P, PASSES, P, PACK], BF16, align_bytes=64, name="xg")
+            xg[m] = consts.tile([P, PASSES, P, PACK], BF16, align_bytes=64, name="xg%d" % m)
             nc.scalar.copy(
                 out=xg[m][:]
                 .rearrange("p g r t -> p (g r t)")
@@ -234,81 +236,138 @@ def tile_ltransformerdecoderblock_pa_kernel(
         def quantise_unit(w, u):
             quantise_columns(w, u, 0, N_TILE)
 
-        steps = [(w, m) for w in range(len(weights)) for m in range(TOKEN_TILES)]
-        banks = [(i, h) for i in range(len(steps)) for h in range(HALVES)]
-        issued = []
-        acc = {}
-        o_sb = {}
+        def bank_parts(b):
+            i, h = divmod(b, HALVES)
+            w, m = divmod(i, TOKEN_TILES)
+            return w, m, h
 
-        def matmuls(last_step):
-            for i, h in banks[len(issued) :]:
-                w, m = steps[i]
-                units = [g * HALVES + h for g in range(PASSES)]
-                if i > last_step or any((w, u) not in quantised for u in units):
+        unwritten = list(range(len(weights) * TOKEN_TILES * HALVES))
+        filled = []
+        acc = {}
+
+        def matmuls():
+            while len(filled) < AHEAD:
+                ready = [
+                    b
+                    for b in unwritten
+                    if bank_parts(b)[1] in x_codes
+                    and all(
+                        (bank_parts(b)[0], g * HALVES + bank_parts(b)[2]) in quantised
+                        for g in range(PASSES)
+                    )
+                ]
+                if not ready:
                     return
-                issued.append((i, h))
-                acc[(i, h)] = psum.tile([P, N_TILE], F32, tag="bank", name="acc")
+                b = ready[0]
+                w, m, h = bank_parts(b)
+                unwritten.remove(b)
+                filled.append(b)
+                acc[b] = psum.tile([P, N_TILE], F32, tag="bank", name="acc")
                 for g in range(PASSES):
                     nc.tensor.matmul_mx(
-                        out=acc[(i, h)][:],
+                        out=acc[b][:],
                         lhsT=x_codes[m][:, g * P : (g + 1) * P].bitcast(FP8X4),
                         lhsT_scale=x_scales[m][:, g * P : (g + 1) * P],
-                        rhs=w_codes[(w, units[g])][:].bitcast(FP8X4),
-                        rhs_scale=w_scales[(w, units[g])][:],
+                        rhs=w_codes[(w, g * HALVES + h)][:].bitcast(FP8X4),
+                        rhs_scale=w_scales[(w, g * HALVES + h)][:],
                         start=(g == 0),
                         stop=(g == PASSES - 1),
                     )
 
-        def copy_out(i, h):
-            if h == 0:
-                o_sb[i] = opool.tile([P, H, HD + 1], F32, name="o_sb")
-            first = h * HEADS_PER_BANK
-            nc.scalar.copy(
-                out=o_sb[i][:, first : first + HEADS_PER_BANK, 1:],
-                in_=acc[(i, h)][:].rearrange("p (a c) -> p a c", c=HD),
-            )
-
-        def head_stats(stats, k, i, h):
-            for j in range(HEADS_PER_BANK // 2):
-                first = h * HEADS_PER_BANK + 2 * j
+        def head_stats(stats, j, b):
+            for q in range(HEADS_PER_BANK // 2):
                 nc.vector.bn_stats(
-                    out=stats[:, k, first : first + 2, :].rearrange("p a s -> p (a s)"),
-                    in_=acc[(i, h)][:, 2 * j * HD : (2 * j + 2) * HD].rearrange(
+                    out=stats[:, j, 2 * q : 2 * q + 2, :].rearrange("p a s -> p (a s)"),
+                    in_=acc[b][:, 2 * q * HD : (2 * q + 2) * HD].rearrange(
                         "p (a c) -> p c a", a=2
                     ),
                 )
 
-        def new_stats(count):
-            return opool.tile([P, count, H, 3], F32, name="stats")
-
-        def square_means(stats, count):
-            mean_sq = opool.tile([P, count, H], F32, name="mean_sq")
-            nc.vector.tensor_tensor(
-                out=mean_sq[:], in0=stats[:, :, :, 1], in1=stats[:, :, :, 1], op=ALU.mult
+        def copy_out(lifted, j, b):
+            nc.scalar.copy(
+                out=lifted[:, j, :, 1:], in_=acc[b][:].rearrange("p (a c) -> p a c", c=HD)
             )
-            return mean_sq
 
-        def sum_heads(stats, mean_sq, count):
-            head_sumsq = opool.tile([P, count, H], F32, name="head_sumsq")
+        slots = []
+
+        def new_slot(count):
+            s = len(slots)
+            slots.append(
+                {
+                    "banks": [],
+                    "lifted": opool.tile(
+                        [P, count, HEADS_PER_BANK, HD + 1], F32, name="lifted%d" % s
+                    ),
+                    "stats": opool.tile([P, count, HEADS_PER_BANK, 3], F32, name="stats%d" % s),
+                    "mean_sq": opool.tile([P, count, HEADS_PER_BANK], F32, name="mean_sq%d" % s),
+                    "sumsq": opool.tile([P, count, HEADS_PER_BANK], F32, name="sumsq_h%d" % s),
+                }
+            )
+            return slots[s]
+
+        def read_bank(slot):
+            matmuls()
+            b = filled[0]
+            filled.remove(b)
+            j = len(slot["banks"])
+            slot["banks"].append(b)
+            head_stats(slot["stats"], j, b)
+            matmuls()
+            copy_out(slot["lifted"], j, b)
+
+        def square_means(slot):
+            nc.vector.tensor_tensor(
+                out=slot["mean_sq"][:],
+                in0=slot["stats"][:, :, :, 1],
+                in1=slot["stats"][:, :, :, 1],
+                op=ALU.mult,
+            )
+
+        def sum_heads(slot):
             nc.vector.scalar_tensor_tensor(
-                out=head_sumsq[:],
-                in0=mean_sq[:],
+                out=slot["sumsq"][:],
+                in0=slot["mean_sq"][:],
                 scalar=float(HD),
-                in1=stats[:, :, :, 2],
+                in1=slot["stats"][:, :, :, 2],
                 op0=ALU.mult,
                 op1=ALU.add,
             )
-            return head_sumsq
 
-        def lift_and_store(head_sumsq, k, i):
-            w, m = steps[i]
+        def lift_and_store(slot):
             nc.scalar.activation(
-                out=o_sb[i][:, :, 0], in_=head_sumsq[:, k, :], func=ACT.Sqrt, bias=1.0 / CURV
+                out=slot["lifted"][:, :, :, 0],
+                in_=slot["sumsq"][:],
+                func=ACT.Sqrt,
+                bias=1.0 / CURV,
             )
-            nc.sync.dma_start(
-                out=outputs[w][m * P : (m + 1) * P, :],
-                in_=o_sb[i][:].rearrange("p h c -> p (h c)"),
+            width = HEADS_PER_BANK * (HD + 1)
+            for j, b in enumerate(slot["banks"]):
+                w, m, h = bank_parts(b)
+                nc.sync.dma_start(
+                    out=outputs[w][m * P : (m + 1) * P, h * width : (h + 1) * width],
+                    in_=slot["lifted"][:, j].rearrange("p a c -> p (a c)"),
+                )
+
+        def close_slot(slot, first, second, others):
+            first()
+            square_means(slot)
+            second()
+            sum_heads(slot)
+            for other in others:
+                other()
+            matmuls()
+            open_gate()
+
+        def unit_quantiser(unit):
+            return lambda: quantise_unit(unit[0], unit[1])
+
+        def half_quantiser(unit, half):
+            return lambda: quantise_columns(
+                unit[0], unit[1], half * (N_TILE // 2), (half + 1) * (N_TILE // 2)
             )
+
+        def token_quantiser(m):
+            return lambda: quantise_tokens(m)
 
         root_mean_square(0)
         reciprocal(0)
@@ -321,82 +380,81 @@ def tile_ltransformerdecoderblock_pa_kernel(
         copy_tokens(0)
         root_mean_square(3)
         copy_tokens(1)
-        reciprocal(2)
-        norm_transpose(2)
 
         quantise_unit(0, 0)
-        quantise_tokens(0)
-        quantise_tokens(1)
-        reciprocal(3)
+        reciprocal(2)
         open_gate()
 
         regroup("gpsimd", 0, 2)
+        norm_transpose(2, between=3)
+        norm_transpose(3)
         root_mean_square(4)
         copy_tokens(2)
-        regroup("scalar", 0, 1)
-        norm_transpose(3, between=4)
-        norm_transpose(4)
         copy_tokens(3)
-        copy_tokens(4)
-        regroup("scalar", 1, 1)
+        regroup("scalar", 0, 1)
 
         quantise_unit(0, 2)
-        matmuls(1)
-        regroup("vector", 0, 3)
-        quantise_unit(0, 1)
-        quantise_tokens(2)
-        quantise_unit(0, 3)
-        matmuls(1)
-        quantise_tokens(3)
-        quantise_tokens(4)
+        for m in range(3):
+            quantise_tokens(m)
+        reciprocal(4)
+        matmuls()
         open_gate()
 
-        gpsimd_units = [(1, 0), (1, 2), (2, 0), (2, 2), (2, 1)]
-        scalar_units = {0: (1, 3), 2: (2, 3)}
-        scalar_ready = {0: (1, 1), 1: (1, 3), 3: (2, 3)}
-        to_lift = []
-        for s in range(len(gpsimd_units)):
-            regroup("gpsimd", gpsimd_units[s][0], gpsimd_units[s][1])
-            stats = new_stats(2)
-            for k in range(2):
-                i = 2 * s + k
-                matmuls(i + AHEAD)
-                for h in range(HALVES):
-                    head_stats(stats, k, i, h)
-                    copy_out(i, h)
-                if k == 0:
-                    for sums, kk, ii in to_lift:
-                        lift_and_store(sums, kk, ii)
-                    to_lift = []
-                    if s in scalar_units:
-                        regroup("scalar", scalar_units[s][0], scalar_units[s][1])
-            if s in scalar_ready:
-                quantise_unit(scalar_ready[s][0], scalar_ready[s][1])
-                mean_sq = square_means(stats, 2)
-                quantise_unit(gpsimd_units[s][0], gpsimd_units[s][1])
-            else:
-                quantise_columns(gpsimd_units[s][0], gpsimd_units[s][1], 0, N_TILE // 2)
-                mean_sq = square_means(stats, 2)
-                quantise_columns(gpsimd_units[s][0], gpsimd_units[s][1], N_TILE // 2, N_TILE)
-            head_sumsq = sum_heads(stats, mean_sq, 2)
-            open_gate()
-            to_lift = [(head_sumsq, 0, 2 * s), (head_sumsq, 1, 2 * s + 1)]
+        regroup("gpsimd", 0, 3)
+        norm_transpose(4)
+        copy_tokens(4)
+        slot = new_slot(FIRST_BANKS)
+        for j in range(FIRST_BANKS):
+            read_bank(slot)
+        close_slot(
+            slot,
+            unit_quantiser((0, 1)),
+            unit_quantiser((0, 3)),
+            [token_quantiser(3), token_quantiser(4)],
+        )
+        lift_and_store(slot)
+        regroup("scalar", 1, 2)
 
-        before = None
-        for i in range(2 * len(gpsimd_units), len(steps)):
-            matmuls(i + AHEAD)
-            stats = new_stats(1)
-            head_stats(stats, 0, i, 0)
-            copy_out(i, 0)
-            if before is not None:
-                mean_sq = square_means(before[0], 1)
-            head_stats(stats, 0, i, 1)
-            copy_out(i, 1)
-            if before is not None:
-                lift_and_store(sum_heads(before[0], mean_sq, 1), 0, before[1])
-            for sums, kk, ii in to_lift:
-                lift_and_store(sums, kk, ii)
-            to_lift = []
-            before = (stats, i)
-        mean_sq = square_means(before[0], 1)
-        lift_and_store(sum_heads(before[0], mean_sq, 1), 0, before[1])
+        plan = [
+            ((1, 0), (1, 3), (1, 2), None),
+            ((1, 1), (2, 2), (1, 3), None),
+            ((2, 0), None, (2, 2), (2, 3)),
+            ((2, 1), None, None, None),
+        ]
+        for gpsimd_unit, scalar_unit, scalar_done, vector_unit in plan:
+            regroup("gpsimd", gpsimd_unit[0], gpsimd_unit[1])
+            slot = new_slot(SLOT_BANKS)
+            for j in range(SLOT_BANKS):
+                read_bank(slot)
+                if j == 1 and scalar_unit is not None:
+                    regroup("scalar", scalar_unit[0], scalar_unit[1])
+            if vector_unit is not None:
+                regroup("vector", vector_unit[0], vector_unit[1])
+            if scalar_done is not None:
+                close_slot(
+                    slot,
+                    unit_quantiser(scalar_done),
+                    unit_quantiser(gpsimd_unit),
+                    [unit_quantiser(vector_unit)] if vector_unit is not None else [],
+                )
+            else:
+                close_slot(
+                    slot, half_quantiser(gpsimd_unit, 0), half_quantiser(gpsimd_unit, 1), []
+                )
+            lift_and_store(slot)
+
+        small_due = []
+        while unwritten or filled:
+            slot = new_slot(min(2, len(unwritten) + len(filled)))
+            read_bank(slot)
+            for due in small_due:
+                square_means(due)
+            if unwritten or filled:
+                read_bank(slot)
+            for due in small_due:
+                sum_heads(due)
+                lift_and_store(due)
+            small_due = [slot]
+        square_means(slot)
+        sum_heads(slot)
+        lift_and_store(slot)

@@ -341,12 +341,30 @@ def tile_ltransformerdecoderblock_pa_kernel(
                 bias=1.0 / CURV,
             )
             width = HEADS_PER_BANK * (HD + 1)
-            for j, b in enumerate(slot["banks"]):
-                w, m, h = bank_parts(b)
-                nc.sync.dma_start(
-                    out=outputs[w][m * P : (m + 1) * P, h * width : (h + 1) * width],
-                    in_=slot["lifted"][:, j].rearrange("p a c -> p (a c)"),
-                )
+            banks = slot["banks"]
+            j = 0
+            while j < len(banks):
+                w, m, h = bank_parts(banks[j])
+                count = 1
+                if h == 0 and banks[j + 1 : j + 2] == [banks[j] + 1]:
+                    count = HALVES
+                    nc.sync.dma_start(
+                        out=outputs[w][m * P : (m + 1) * P, :],
+                        in_=slot["lifted"][:, j : j + count].rearrange("p j a c -> p (j a c)"),
+                    )
+                else:
+                    while (
+                        m + count < TOKEN_TILES
+                        and banks[j + count : j + count + 1] == [banks[j] + HALVES * count]
+                    ):
+                        count += 1
+                    nc.sync.dma_start(
+                        out=outputs[w][
+                            m * P : (m + count) * P, h * width : (h + 1) * width
+                        ].rearrange("(m p) c -> p m c", p=P),
+                        in_=slot["lifted"][:, j : j + count].rearrange("p j a c -> p j (a c)"),
+                    )
+                j += count
 
         def close_slot(slot, first, second, others):
             first()

@@ -410,6 +410,7 @@ def tile_ltransformerdecoderblock_pa_kernel(
         copy_tokens(2)
         copy_tokens(3)
         regroup("scalar", 0, 1)
+        regroup("scalar", 1, 2)
 
         quantise_unit(0, 2)
         for m in range(3):
@@ -431,7 +432,6 @@ def tile_ltransformerdecoderblock_pa_kernel(
             [token_quantiser(3), token_quantiser(4)],
         )
         lift_and_store(slot)
-        regroup("scalar", 1, 2)
 
         plan = [
             ((1, 0), (1, 3), (1, 2), None),

@@ -31,6 +31,8 @@ AHEAD = 3
 SLOT_BANKS = 5
 FIRST_BANKS = 3
 
+IDLE_MATMULS = 2
+
 FLOPS = 2 * TOKENS * D * 3 * E
 
 
@@ -124,6 +126,14 @@ def tile_ltransformerdecoderblock_pa_kernel(
                 stop=True,
             )
             gain_all.append(spread)
+
+        idle_bank = psum.tile([P, N_TILE], F32, tag="bank", name="idle_bank")
+
+        def keep_tensor_busy():
+            for c in range(IDLE_MATMULS):
+                nc.tensor.matmul(
+                    out=idle_bank[:], lhsT=ones[:], rhs=gain_row[:, :N_TILE], start=True, stop=True
+                )
 
         rms = {}
         rstd = {}
@@ -367,6 +377,7 @@ def tile_ltransformerdecoderblock_pa_kernel(
                 j += count
 
         def close_slot(slot, first, second, others):
+            keep_tensor_busy()
             first()
             square_means(slot)
             second()
@@ -412,6 +423,7 @@ def tile_ltransformerdecoderblock_pa_kernel(
         regroup("scalar", 0, 1)
         regroup("scalar", 1, 2)
 
+        keep_tensor_busy()
         quantise_unit(0, 2)
         for m in range(3):
             quantise_tokens(m)

@@ -129,10 +129,14 @@ def tile_ltransformerdecoderblock_pa_kernel(
 
         idle_bank = psum.tile([P, N_TILE], F32, tag="bank", name="idle_bank")
 
-        def keep_tensor_busy():
+        def keep_tensor_busy(unit):
             for c in range(IDLE_MATMULS):
                 nc.tensor.matmul(
-                    out=idle_bank[:], lhsT=ones[:], rhs=gain_row[:, :N_TILE], start=True, stop=True
+                    out=idle_bank[:],
+                    lhsT=ones[:],
+                    rhs=wg[unit][:, : N_TILE // PACK, :].rearrange("p n t -> p (n t)"),
+                    start=True,
+                    stop=True,
                 )
 
         rms = {}
@@ -376,8 +380,9 @@ def tile_ltransformerdecoderblock_pa_kernel(
                     )
                 j += count
 
-        def close_slot(slot, first, second, others):
-            keep_tensor_busy()
+        def close_slot(slot, regrouped, first, second, others):
+            for unit in regrouped:
+                keep_tensor_busy(unit)
             first()
             square_means(slot)
             second()
@@ -423,7 +428,7 @@ def tile_ltransformerdecoderblock_pa_kernel(
         regroup("scalar", 0, 1)
         regroup("scalar", 1, 2)
 
-        keep_tensor_busy()
+        keep_tensor_busy((0, 2))
         quantise_unit(0, 2)
         for m in range(3):
             quantise_tokens(m)
@@ -439,6 +444,7 @@ def tile_ltransformerdecoderblock_pa_kernel(
             read_bank(slot)
         close_slot(
             slot,
+            [(0, 3)],
             unit_quantiser((0, 1)),
             unit_quantiser((0, 3)),
             [token_quantiser(3), token_quantiser(4)],
@@ -463,13 +469,18 @@ def tile_ltransformerdecoderblock_pa_kernel(
             if scalar_done is not None:
                 close_slot(
                     slot,
+                    [gpsimd_unit] + ([vector_unit] if vector_unit is not None else []),
                     unit_quantiser(scalar_done),
                     unit_quantiser(gpsimd_unit),
                     [unit_quantiser(vector_unit)] if vector_unit is not None else [],
                 )
             else:
                 close_slot(
-                    slot, half_quantiser(gpsimd_unit, 0), half_quantiser(gpsimd_unit, 1), []
+                    slot,
+                    [gpsimd_unit],
+                    half_quantiser(gpsimd_unit, 0),
+                    half_quantiser(gpsimd_unit, 1),
+                    [],
                 )
             lift_and_store(slot)
 

@@ -10,6 +10,7 @@ U8 = mybir.dt.uint8
 FP8X4 = mybir.dt.float8_e4m3fn_x4
 ACT = mybir.ActivationFunctionType
 ALU = mybir.AluOpType
+AX = mybir.AxisListType
 
 P = 128
 PACK = 4
@@ -26,12 +27,10 @@ TOKEN_TILES = TOKENS // P
 N_TILE = 512
 HALVES = E // N_TILE
 HEADS_PER_BANK = N_TILE // HD
+BANKS = 8
 RUN = 4
+TENSOR_COLS = 1024 // PACK
 AHEAD = 3
-SLOT_BANKS = 5
-FIRST_BANKS = 3
-
-IDLE_MATMULS = 2
 
 FLOPS = 2 * TOKENS * D * 3 * E
 
@@ -49,8 +48,18 @@ def tile_ltransformerdecoderblock_pa_kernel(
         xwork = ctx.enter_context(tc.tile_pool(name="xwork", bufs=3))
         wwork = ctx.enter_context(tc.tile_pool(name="wwork", bufs=2))
         opool = ctx.enter_context(tc.tile_pool(name="opool", bufs=1))
-        psum = ctx.enter_context(tc.psum_pool(name="psum", bufs=8))
+        psum = ctx.enter_context(tc.psum_pool(name="psum", bufs=1))
         ctx.enter_context(tc.manual_schedule())
+
+        rotation = {"next": 0, "first": 2}
+
+        def bank_tile(shape, dtype):
+            b = rotation["next"]
+            if b < rotation["first"]:
+                b = rotation["first"]
+            rotation["next"] = (b + 1) % BANKS
+            fresh = psum.tile(shape, dtype, tag="bank%d" % b, name="bank%d" % b)
+            return fresh
 
         one = consts.tile([P, 1], F32)
         nc.vector.memset(one[:], 1.0)
@@ -64,13 +73,13 @@ def tile_ltransformerdecoderblock_pa_kernel(
 
         ident = consts.tile([P, P], F32)
         make_identity(nc, ident[:])
+        ident_bf = consts.tile([P, P], BF16)
+        nc.vector.tensor_copy(out=ident_bf[:], in_=ident[:])
 
         token = consts.tile([P, 1], F32)
 
         def open_gate():
             nc.vector.memset(token[:], 1.0)
-
-        open_gate()
 
         x_sb = []
         raw = {}
@@ -104,11 +113,11 @@ def tile_ltransformerdecoderblock_pa_kernel(
         load_tokens(0)
         nc.sync.dma_start(out=gain_row[0:1, :], in_=ln1_w.rearrange("(o d) -> o d", o=1))
         load_tokens(1)
-        load_unit(0, 0)
         load_tokens(2)
-        load_unit(0, 2)
+        load_unit(0, 0)
         load_tokens(3)
         load_tokens(4)
+        load_unit(0, 2)
         load_unit(0, 1)
         load_unit(0, 3)
         for w in range(1, len(weights)):
@@ -117,7 +126,7 @@ def tile_ltransformerdecoderblock_pa_kernel(
 
         gain_all = []
         for h in range(D // N_TILE):
-            spread = psum.tile([P, N_TILE], F32, tag="bank", name="spread")
+            spread = psum.tile([P, N_TILE], F32, tag="bank%d" % h, name="spread%d" % h)
             nc.tensor.matmul(
                 out=spread[:],
                 lhsT=ones[:],
@@ -127,18 +136,7 @@ def tile_ltransformerdecoderblock_pa_kernel(
             )
             gain_all.append(spread)
 
-        idle_bank = psum.tile([P, N_TILE], F32, tag="bank", name="idle_bank")
-
-        def keep_tensor_busy(unit):
-            for c in range(IDLE_MATMULS):
-                nc.tensor.matmul(
-                    out=idle_bank[:],
-                    lhsT=ones[:],
-                    rhs=wg[unit][:, : N_TILE // PACK, :].rearrange("p n t -> p (n t)"),
-                    start=True,
-                    stop=True,
-                )
-
+        sumsq = {}
         rms = {}
         rstd = {}
         xt = {}
@@ -146,15 +144,28 @@ def tile_ltransformerdecoderblock_pa_kernel(
         x_codes = {}
         x_scales = {}
 
-        def root_mean_square(m):
-            squares = xwork.tile([P, D], BF16)
-            sumsq = consts.tile([P, 1], F32, name="sumsq%d" % m)
-            nc.scalar.activation(
-                out=squares[:], in_=x_sb[m][:], func=ACT.Square, accum_out=sumsq[:]
-            )
+        def sum_squares(engine, m):
+            squares = xwork.tile([P, D], BF16, name="squares")
+            sumsq[m] = consts.tile([P, 1], F32, name="sumsq%d" % m)
+            if engine == "scalar":
+                nc.scalar.activation(
+                    out=squares[:], in_=x_sb[m][:], func=ACT.Square, accum_out=sumsq[m][:]
+                )
+            else:
+                nc.vector.scalar_tensor_tensor(
+                    out=squares[:],
+                    in0=x_sb[m][:],
+                    scalar=1.0,
+                    in1=x_sb[m][:],
+                    op0=ALU.mult,
+                    op1=ALU.mult,
+                    accum_out=sumsq[m][:],
+                )
+
+        def root(m):
             rms[m] = consts.tile([P, 1], F32, name="rms%d" % m)
             nc.scalar.activation(
-                out=rms[m][:], in_=sumsq[:], func=ACT.Sqrt, scale=1.0 / D, bias=EPS
+                out=rms[m][:], in_=sumsq[m][:], func=ACT.Sqrt, scale=1.0 / D, bias=EPS
             )
 
         def reciprocal(m):
@@ -162,7 +173,7 @@ def tile_ltransformerdecoderblock_pa_kernel(
             nc.vector.reciprocal(out=rstd[m][:], in_=rms[m][:])
 
         def norm_transpose(m, between=None):
-            normed = xwork.tile([P, D], BF16)
+            normed = xwork.tile([P, D], BF16, name="normed")
             for h in range(D // N_TILE):
                 cols = slice(h * N_TILE, (h + 1) * N_TILE)
                 nc.vector.scalar_tensor_tensor(
@@ -176,7 +187,7 @@ def tile_ltransformerdecoderblock_pa_kernel(
                 if h == 0 and between is not None:
                     reciprocal(between)
             words = normed[:].bitcast(F32)
-            xt[m] = psum.tile([P, PASSES, 2, P], F32, tag="bank", name="xt")
+            xt[m] = bank_tile([P, PASSES, 2, P], F32)
             for g in range(PASSES):
                 for u in range(2):
                     nc.tensor.transpose(
@@ -205,78 +216,85 @@ def tile_ltransformerdecoderblock_pa_kernel(
             )
 
         wg = {}
+        turned = {}
         w_codes = {}
         w_scales = {}
         quantised = set()
 
-        def regroup(engine, w, u):
-            source = raw[(w, u)][:, :, :]
-            if engine == "gpsimd":
-                wg[(w, u)] = wwork.tile([P, N_TILE, PACK], BF16, align_bytes=64, name="wg_g")
-                nc.gpsimd.tensor_scalar(
-                    out=wg[(w, u)][:],
-                    in0=source.rearrange("p t c -> p c t"),
-                    scalar1=token[:],
-                    scalar2=0.0,
-                    op0=ALU.mult,
-                    op1=ALU.add,
-                )
-                return
-            name = "wg_s" if engine == "scalar" else "wg_v"
-            wg[(w, u)] = wwork.tile([P, N_TILE, PACK], BF16, align_bytes=64, name=name)
-            dst = wg[(w, u)][:].rearrange("p (c i) t -> p c t i", i=RUN)
-            src = source.rearrange("p t (c i) -> p c t i", i=RUN)
-            if engine == "scalar":
-                nc.scalar.copy(out=dst, in_=src)
-            else:
-                nc.vector.tensor_copy(out=dst, in_=src)
-
-        def quantise_columns(w, u, lo, hi):
-            if lo == 0:
-                w_codes[(w, u)] = consts.tile(
-                    [P, N_TILE], U32, name="wc%d_%d" % (w, u), align_bytes=64
-                )
-                w_scales[(w, u)] = consts.tile(
-                    [P, N_TILE], U8, name="wsc%d_%d" % (w, u), align_bytes=64
-                )
-            nc.vector.quantize_mx(
-                out=w_codes[(w, u)][:, lo:hi].bitcast(FP8X4),
-                scales=w_scales[(w, u)][:, lo:hi],
-                in_=wg[(w, u)][:, lo:hi, :].rearrange("p n t -> p (n t)"),
+        def regroup_gpsimd(unit):
+            wg[unit] = wwork.tile([P, N_TILE, PACK], BF16, align_bytes=64, name="wg_g")
+            nc.gpsimd.tensor_scalar(
+                out=wg[unit][:],
+                in0=raw[unit][:, :, :].rearrange("p t c -> p c t"),
+                scalar1=token[:],
+                scalar2=0.0,
+                op0=ALU.mult,
+                op1=ALU.add,
             )
-            if hi == N_TILE:
-                quantised.add((w, u))
 
-        def quantise_unit(w, u):
-            quantise_columns(w, u, 0, N_TILE)
+        def regroup_scalar(unit):
+            wg[unit] = wwork.tile([P, N_TILE, PACK], BF16, align_bytes=64, name="wg_s")
+            nc.scalar.copy(
+                out=wg[unit][:].rearrange("p (c i) t -> p c t i", i=RUN),
+                in_=raw[unit][:, :, :].rearrange("p t (c i) -> p c t i", i=RUN),
+            )
+
+        def regroup_tensor(unit):
+            source = raw[unit][:, :, :]
+            turned[unit] = []
+            for c in range(0, N_TILE, TENSOR_COLS):
+                bank = bank_tile([P, TENSOR_COLS, PACK], BF16)
+                for q in range(c, c + TENSOR_COLS, P):
+                    nc.tensor.matmul(
+                        out=bank[:, q - c : q - c + P, :],
+                        lhsT=ident_bf[:],
+                        rhs=source[:, :, q : q + P].rearrange("p t c -> p c t"),
+                        start=True,
+                        stop=True,
+                    )
+                turned[unit].append(bank)
+
+        def copy_unit(unit, b):
+            if b == 0:
+                wg[unit] = wwork.tile(
+                    [P, N_TILE, PACK], BF16, align_bytes=64, bufs=3, name="wg_t"
+                )
+            nc.scalar.copy(
+                out=wg[unit][:, b * TENSOR_COLS : (b + 1) * TENSOR_COLS, :],
+                in_=turned[unit][b][:],
+            )
+
+        def quantise_unit(unit):
+            w, u = unit
+            w_codes[unit] = consts.tile([P, N_TILE], U32, name="wc%d_%d" % (w, u), align_bytes=64)
+            w_scales[unit] = consts.tile([P, N_TILE], U8, name="wsc%d_%d" % (w, u), align_bytes=64)
+            nc.vector.quantize_mx(
+                out=w_codes[unit][:].bitcast(FP8X4),
+                scales=w_scales[unit][:],
+                in_=wg[unit][:].rearrange("p n t -> p (n t)"),
+            )
+            quantised.add(unit)
 
         def bank_parts(b):
-            i, h = divmod(b, HALVES)
-            w, m = divmod(i, TOKEN_TILES)
+            i, m = divmod(b, TOKEN_TILES)
+            w, h = divmod(i, HALVES)
             return w, m, h
 
-        unwritten = list(range(len(weights) * TOKEN_TILES * HALVES))
+        total = len(weights) * HALVES * TOKEN_TILES
         filled = []
         acc = {}
+        order = {"filled": 0, "read": 0}
 
         def matmuls():
-            while len(filled) < AHEAD:
-                ready = [
-                    b
-                    for b in unwritten
-                    if bank_parts(b)[1] in x_codes
-                    and all(
-                        (bank_parts(b)[0], g * HALVES + bank_parts(b)[2]) in quantised
-                        for g in range(PASSES)
-                    )
-                ]
-                if not ready:
-                    return
-                b = ready[0]
+            while order["filled"] < min(order["read"] + AHEAD, total):
+                b = order["filled"]
                 w, m, h = bank_parts(b)
-                unwritten.remove(b)
-                filled.append(b)
-                acc[b] = psum.tile([P, N_TILE], F32, tag="bank", name="acc")
+                if m not in x_codes or any(
+                    (w, g * HALVES + h) not in quantised for g in range(PASSES)
+                ):
+                    return
+                order["filled"] += 1
+                acc[b] = bank_tile([P, N_TILE], F32)
                 for g in range(PASSES):
                     nc.tensor.matmul_mx(
                         out=acc[b][:],
@@ -288,63 +306,53 @@ def tile_ltransformerdecoderblock_pa_kernel(
                         stop=(g == PASSES - 1),
                     )
 
-        def head_stats(stats, j, b):
-            for q in range(HEADS_PER_BANK // 2):
-                nc.vector.bn_stats(
-                    out=stats[:, j, 2 * q : 2 * q + 2, :].rearrange("p a s -> p (a s)"),
-                    in_=acc[b][:, 2 * q * HD : (2 * q + 2) * HD].rearrange(
-                        "p (a c) -> p c a", a=2
-                    ),
-                )
-
-        def copy_out(lifted, j, b):
-            nc.scalar.copy(
-                out=lifted[:, j, :, 1:], in_=acc[b][:].rearrange("p (a c) -> p a c", c=HD)
-            )
-
         slots = []
 
         def new_slot(count):
             s = len(slots)
             slots.append(
                 {
+                    "count": count,
                     "banks": [],
                     "lifted": opool.tile(
                         [P, count, HEADS_PER_BANK, HD + 1], F32, name="lifted%d" % s
                     ),
                     "stats": opool.tile([P, count, HEADS_PER_BANK, 3], F32, name="stats%d" % s),
-                    "mean_sq": opool.tile([P, count, HEADS_PER_BANK], F32, name="mean_sq%d" % s),
                     "sumsq": opool.tile([P, count, HEADS_PER_BANK], F32, name="sumsq_h%d" % s),
                 }
             )
             return slots[s]
 
-        def read_bank(slot):
-            matmuls()
-            b = filled[0]
-            filled.remove(b)
+        def head_stats(slot):
+            b = order["read"]
+            order["read"] += 1
             j = len(slot["banks"])
             slot["banks"].append(b)
-            head_stats(slot["stats"], j, b)
-            matmuls()
-            copy_out(slot["lifted"], j, b)
+            for q in range(HEADS_PER_BANK // 2):
+                nc.vector.bn_stats(
+                    out=slot["stats"][:, j, 2 * q : 2 * q + 2, :].rearrange("p a s -> p (a s)"),
+                    in_=acc[b][:, 2 * q * HD : (2 * q + 2) * HD].rearrange(
+                        "p (a c) -> p c a", a=2
+                    ),
+                )
+
+        def copy_out(slot, j):
+            nc.scalar.copy(
+                out=slot["lifted"][:, j, :, 1:],
+                in_=acc[slot["banks"][j]][:].rearrange("p (a c) -> p a c", c=HD),
+            )
 
         def square_means(slot):
-            nc.vector.tensor_tensor(
-                out=slot["mean_sq"][:],
-                in0=slot["stats"][:, :, :, 1],
-                in1=slot["stats"][:, :, :, 1],
-                op=ALU.mult,
+            nc.scalar.activation(
+                out=slot["stats"][:, :, :, 1],
+                in_=slot["stats"][:, :, :, 1],
+                func=ACT.Square,
+                scale=float(HD) ** 0.5,
             )
 
         def sum_heads(slot):
-            nc.vector.scalar_tensor_tensor(
-                out=slot["sumsq"][:],
-                in0=slot["mean_sq"][:],
-                scalar=float(HD),
-                in1=slot["stats"][:, :, :, 2],
-                op0=ALU.mult,
-                op1=ALU.add,
+            nc.vector.tensor_reduce(
+                out=slot["sumsq"][:], in_=slot["stats"][:, :, :, 1:], op=ALU.add, axis=AX.X
             )
 
         def lift_and_store(slot):
@@ -355,147 +363,107 @@ def tile_ltransformerdecoderblock_pa_kernel(
                 bias=1.0 / CURV,
             )
             width = HEADS_PER_BANK * (HD + 1)
-            banks = slot["banks"]
-            j = 0
-            while j < len(banks):
-                w, m, h = bank_parts(banks[j])
-                count = 1
-                if h == 0 and banks[j + 1 : j + 2] == [banks[j] + 1]:
-                    count = HALVES
-                    nc.sync.dma_start(
-                        out=outputs[w][m * P : (m + 1) * P, :],
-                        in_=slot["lifted"][:, j : j + count].rearrange("p j a c -> p (j a c)"),
-                    )
-                else:
-                    while (
-                        m + count < TOKEN_TILES
-                        and banks[j + count : j + count + 1] == [banks[j] + HALVES * count]
-                    ):
-                        count += 1
-                    nc.sync.dma_start(
-                        out=outputs[w][
-                            m * P : (m + count) * P, h * width : (h + 1) * width
-                        ].rearrange("(m p) c -> p m c", p=P),
-                        in_=slot["lifted"][:, j : j + count].rearrange("p j a c -> p j (a c)"),
-                    )
-                j += count
-
-        def close_slot(slot, regrouped, first, second, others):
-            for unit in regrouped:
-                keep_tensor_busy(unit)
-            first()
-            square_means(slot)
-            second()
-            sum_heads(slot)
-            for other in others:
-                other()
-            matmuls()
-            open_gate()
-
-        def unit_quantiser(unit):
-            return lambda: quantise_unit(unit[0], unit[1])
-
-        def half_quantiser(unit, half):
-            return lambda: quantise_columns(
-                unit[0], unit[1], half * (N_TILE // 2), (half + 1) * (N_TILE // 2)
+            w, m, h = bank_parts(slot["banks"][0])
+            count = len(slot["banks"])
+            nc.sync.dma_start(
+                out=outputs[w][m * P : (m + count) * P, h * width : (h + 1) * width].rearrange(
+                    "(m p) c -> p m c", p=P
+                ),
+                in_=slot["lifted"][:].rearrange("p j a c -> p j (a c)"),
             )
 
-        def token_quantiser(m):
-            return lambda: quantise_tokens(m)
+        state = {"slot": None, "due": None, "sizes": [], "behind": 1}
 
-        root_mean_square(0)
+        def read_bank():
+            if state["slot"] is None:
+                state["slot"] = new_slot(state["sizes"].pop(0))
+            slot = state["slot"]
+            matmuls()
+            head_stats(slot)
+            matmuls()
+            j = len(slot["banks"]) - 1
+            if state["due"] is not None and j == min(state["behind"], slot["count"] - 1):
+                sum_heads(state["due"])
+            full = len(slot["banks"]) == slot["count"]
+            if full:
+                square_means(slot)
+            copy_out(slot, j)
+            if state["due"] is not None and j == min(state["behind"], slot["count"] - 1):
+                lift_and_store(state["due"])
+                state["due"] = None
+            if full:
+                state["due"] = slot
+                state["slot"] = None
+
+        sum_squares("scalar", 0)
+        root(0)
+        sum_squares("vector", 1)
+        open_gate()
+        regroup_gpsimd((0, 0))
+        regroup_gpsimd((0, 2))
         reciprocal(0)
-        root_mean_square(1)
-        regroup("gpsimd", 0, 0)
+        sum_squares("scalar", 2)
+        root(1)
         norm_transpose(0)
         reciprocal(1)
-        norm_transpose(1)
-        root_mean_square(2)
+        sum_squares("scalar", 3)
+        root(2)
+        norm_transpose(1, between=2)
+        sum_squares("scalar", 4)
+        root(3)
         copy_tokens(0)
-        root_mean_square(3)
-        copy_tokens(1)
-
-        quantise_unit(0, 0)
-        reciprocal(2)
-        open_gate()
-
-        regroup("gpsimd", 0, 2)
         norm_transpose(2, between=3)
-        norm_transpose(3)
-        root_mean_square(4)
+        regroup_tensor((0, 3))
+        root(4)
+        copy_tokens(1)
+        norm_transpose(3, between=4)
         copy_tokens(2)
+        regroup_scalar((0, 1))
+        norm_transpose(4)
         copy_tokens(3)
-        regroup("scalar", 0, 1)
-        regroup("scalar", 1, 2)
+        copy_tokens(4)
+        regroup_tensor((1, 0))
+        copy_unit((0, 3), 0)
+        copy_unit((0, 3), 1)
 
-        keep_tensor_busy((0, 2))
-        quantise_unit(0, 2)
-        for m in range(3):
-            quantise_tokens(m)
-        reciprocal(4)
+        rotation["first"] = 0
+        quantise_tokens(0)
+        quantise_unit((0, 0))
+        quantise_tokens(1)
+        quantise_unit((0, 2))
         matmuls()
+        quantise_tokens(2)
+        matmuls()
+        copy_unit((1, 0), 0)
+        copy_unit((1, 0), 1)
+        quantise_unit((0, 1))
+        quantise_tokens(3)
+        quantise_tokens(4)
         open_gate()
 
-        regroup("gpsimd", 0, 3)
-        norm_transpose(4)
-        copy_tokens(4)
-        slot = new_slot(FIRST_BANKS)
-        for j in range(FIRST_BANKS):
-            read_bank(slot)
-        close_slot(
-            slot,
-            [(0, 3)],
-            unit_quantiser((0, 1)),
-            unit_quantiser((0, 3)),
-            [token_quantiser(3), token_quantiser(4)],
-        )
-        lift_and_store(slot)
-
+        state["sizes"] = [2, 3] * (len(weights) * HALVES - 1) + [2, 2, 1]
         plan = [
-            ((1, 0), (1, 3), (1, 2), None),
-            ((1, 1), (2, 2), (1, 3), None),
-            ((2, 0), None, (2, 2), (2, 3)),
-            ((2, 1), None, None, None),
+            ((1, 2), (1, 1), [(0, 3), (1, 0), (1, 2)]),
+            ((1, 3), (2, 0), [(1, 1), (1, 3)]),
+            ((2, 2), (2, 1), [(2, 0), (2, 2)]),
+            ((2, 3), None, [(2, 1), (2, 3)]),
         ]
-        for gpsimd_unit, scalar_unit, scalar_done, vector_unit in plan:
-            regroup("gpsimd", gpsimd_unit[0], gpsimd_unit[1])
-            slot = new_slot(SLOT_BANKS)
-            for j in range(SLOT_BANKS):
-                read_bank(slot)
-                if j == 1 and scalar_unit is not None:
-                    regroup("scalar", scalar_unit[0], scalar_unit[1])
-            if vector_unit is not None:
-                regroup("vector", vector_unit[0], vector_unit[1])
-            if scalar_done is not None:
-                close_slot(
-                    slot,
-                    [gpsimd_unit] + ([vector_unit] if vector_unit is not None else []),
-                    unit_quantiser(scalar_done),
-                    unit_quantiser(gpsimd_unit),
-                    [unit_quantiser(vector_unit)] if vector_unit is not None else [],
-                )
-            else:
-                close_slot(
-                    slot,
-                    [gpsimd_unit],
-                    half_quantiser(gpsimd_unit, 0),
-                    half_quantiser(gpsimd_unit, 1),
-                    [],
-                )
-            lift_and_store(slot)
-
-        small_due = []
-        while unwritten or filled:
-            slot = new_slot(min(2, len(unwritten) + len(filled)))
-            read_bank(slot)
-            for due in small_due:
-                square_means(due)
-            if unwritten or filled:
-                read_bank(slot)
-            for due in small_due:
-                sum_heads(due)
-                lift_and_store(due)
-            small_due = [slot]
-        square_means(slot)
-        sum_heads(slot)
-        lift_and_store(slot)
+        for gpsimd_unit, tensor_unit, ready in plan:
+            regroup_gpsimd(gpsimd_unit)
+            for m in range(TOKEN_TILES):
+                if m == TOKEN_TILES - 1 and tensor_unit is not None:
+                    regroup_tensor(tensor_unit)
+                read_bank()
+            for b in range(2):
+                if tensor_unit is not None:
+                    copy_unit(tensor_unit, b)
+            for unit in ready:
+                quantise_unit(unit)
+                matmuls()
+            open_gate()
+        state["behind"] = 0
+        while order["read"] < total:
+            read_bank()
+        last = state["due"]
+        sum_heads(last)
+        lift_and_store(last)

@@ -246,9 +246,9 @@ def tile_ltransformerdecoderblock_pa_kernel(
                 bank = bank_tile([P, TENSOR_COLS, PACK], BF16)
                 for q in range(c, c + TENSOR_COLS, P):
                     nc.tensor.matmul(
-                        out=bank[:, q - c : q - c + P, :],
+                        out=bank[:, q - c : q - c + P, :].rearrange("p c t -> p t c"),
                         lhsT=ident_bf[:],
-                        rhs=source[:, :, q : q + P].rearrange("p t c -> p c t"),
+                        rhs=source[:, :, q : q + P],
                         start=True,
                         stop=True,
                     )

@@ -29,7 +29,10 @@ HALVES = E // N_TILE
 HEADS_PER_BANK = N_TILE // HD
 BANKS = 8
 RUN = 4
+QUARTERS = N_TILE // P
 TENSOR_COLS = 1024 // PACK
+EARLY = 3
+LAST = (2, 2, 1, 2, 2, 1)
 AHEAD = 3
 
 FLOPS = 2 * TOKENS * D * 3 * E
@@ -232,27 +235,31 @@ def tile_ltransformerdecoderblock_pa_kernel(
                 op1=ALU.add,
             )
 
-        def regroup_scalar(unit):
-            wg[unit] = wwork.tile([P, N_TILE, PACK], BF16, align_bytes=64, name="wg_s")
+        def scalar_quarter(unit, q):
+            if q == 0:
+                wg[unit] = wwork.tile(
+                    [P, N_TILE, PACK], BF16, align_bytes=64, bufs=3, name="wg_s"
+                )
+            cols = slice(q * P, (q + 1) * P)
             nc.scalar.copy(
-                out=wg[unit][:].rearrange("p (c i) t -> p c t i", i=RUN),
-                in_=raw[unit][:, :, :].rearrange("p t (c i) -> p c t i", i=RUN),
+                out=wg[unit][:, cols, :].rearrange("p (c i) t -> p c t i", i=RUN),
+                in_=raw[unit][:, :, cols].rearrange("p t (c i) -> p c t i", i=RUN),
             )
 
-        def regroup_tensor(unit):
-            source = raw[unit][:, :, :]
-            turned[unit] = []
-            for c in range(0, N_TILE, TENSOR_COLS):
-                bank = bank_tile([P, TENSOR_COLS, PACK], BF16)
-                for q in range(c, c + TENSOR_COLS, P):
-                    nc.tensor.matmul(
-                        out=bank[:, q - c : q - c + P, :].rearrange("p c t -> p t c"),
-                        lhsT=ident_bf[:],
-                        rhs=source[:, :, q : q + P],
-                        start=True,
-                        stop=True,
-                    )
-                turned[unit].append(bank)
+        def tensor_quarter(unit, q):
+            if q == 0:
+                turned[unit] = []
+            if q % 2 == 0:
+                fresh = bank_tile([P, TENSOR_COLS, PACK], BF16)
+                turned[unit].append(fresh)
+            c = q % 2 * P
+            nc.tensor.matmul(
+                out=turned[unit][q // 2][:, c : c + P, :].rearrange("p c t -> p t c"),
+                lhsT=ident_bf[:],
+                rhs=raw[unit][:, :, q * P : (q + 1) * P],
+                start=True,
+                stop=True,
+            )
 
         def copy_unit(unit, b):
             if b == 0:
@@ -318,17 +325,20 @@ def tile_ltransformerdecoderblock_pa_kernel(
                         [P, count, HEADS_PER_BANK, HD + 1], F32, name="lifted%d" % s
                     ),
                     "stats": opool.tile([P, count, HEADS_PER_BANK, 3], F32, name="stats%d" % s),
+                    "mean_sq": opool.tile([P, count, HEADS_PER_BANK], F32, name="mean_sq%d" % s),
                     "sumsq": opool.tile([P, count, HEADS_PER_BANK], F32, name="sumsq_h%d" % s),
                 }
             )
             return slots[s]
 
-        def head_stats(slot):
+        def head_stats(slot, middle=None):
             b = order["read"]
             order["read"] += 1
             j = len(slot["banks"])
             slot["banks"].append(b)
             for q in range(HEADS_PER_BANK // 2):
+                if q == HEADS_PER_BANK // 4 and middle is not None:
+                    middle()
                 nc.vector.bn_stats(
                     out=slot["stats"][:, j, 2 * q : 2 * q + 2, :].rearrange("p a s -> p (a s)"),
                     in_=acc[b][:, 2 * q * HD : (2 * q + 2) * HD].rearrange(
@@ -343,16 +353,21 @@ def tile_ltransformerdecoderblock_pa_kernel(
             )
 
         def square_means(slot):
-            nc.scalar.activation(
-                out=slot["stats"][:, :, :, 1],
-                in_=slot["stats"][:, :, :, 1],
-                func=ACT.Square,
-                scale=float(HD) ** 0.5,
+            nc.vector.tensor_tensor(
+                out=slot["mean_sq"][:],
+                in0=slot["stats"][:, :, :, 1],
+                in1=slot["stats"][:, :, :, 1],
+                op=ALU.mult,
             )
 
         def sum_heads(slot):
-            nc.vector.tensor_reduce(
-                out=slot["sumsq"][:], in_=slot["stats"][:, :, :, 1:], op=ALU.add, axis=AX.X
+            nc.vector.scalar_tensor_tensor(
+                out=slot["sumsq"][:],
+                in0=slot["mean_sq"][:],
+                scalar=float(HD),
+                in1=slot["stats"][:, :, :, 2],
+                op0=ALU.mult,
+                op1=ALU.add,
             )
 
         def lift_and_store(slot):
@@ -372,28 +387,26 @@ def tile_ltransformerdecoderblock_pa_kernel(
                 in_=slot["lifted"][:].rearrange("p j a c -> p j (a c)"),
             )
 
-        state = {"slot": None, "due": None, "sizes": [], "behind": 1}
+        def scalar_square_means(slot):
+            nc.scalar.activation(
+                out=slot["stats"][:, :, :, 1],
+                in_=slot["stats"][:, :, :, 1],
+                func=ACT.Square,
+                scale=float(HD) ** 0.5,
+            )
 
-        def read_bank():
-            if state["slot"] is None:
-                state["slot"] = new_slot(state["sizes"].pop(0))
-            slot = state["slot"]
+        def add_pairs(slot):
+            nc.vector.tensor_reduce(
+                out=slot["sumsq"][:], in_=slot["stats"][:, :, :, 1:], op=ALU.add, axis=AX.X
+            )
+
+        def read_bank(slot, middle=None, before_copy=None):
             matmuls()
-            head_stats(slot)
+            head_stats(slot, middle)
             matmuls()
-            j = len(slot["banks"]) - 1
-            if state["due"] is not None and j == min(state["behind"], slot["count"] - 1):
-                sum_heads(state["due"])
-            full = len(slot["banks"]) == slot["count"]
-            if full:
-                square_means(slot)
-            copy_out(slot, j)
-            if state["due"] is not None and j == min(state["behind"], slot["count"] - 1):
-                lift_and_store(state["due"])
-                state["due"] = None
-            if full:
-                state["due"] = slot
-                state["slot"] = None
+            if before_copy is not None:
+                before_copy()
+            copy_out(slot, len(slot["banks"]) - 1)
 
         sum_squares("scalar", 0)
         root(0)
@@ -413,18 +426,17 @@ def tile_ltransformerdecoderblock_pa_kernel(
         root(3)
         copy_tokens(0)
         norm_transpose(2, between=3)
-        regroup_tensor((0, 3))
         root(4)
         copy_tokens(1)
         norm_transpose(3, between=4)
         copy_tokens(2)
-        regroup_scalar((0, 1))
+        for q in range(QUARTERS):
+            scalar_quarter((0, 1), q)
         norm_transpose(4)
         copy_tokens(3)
         copy_tokens(4)
-        regroup_tensor((1, 0))
-        copy_unit((0, 3), 0)
-        copy_unit((0, 3), 1)
+        for q in range(QUARTERS):
+            scalar_quarter((0, 3), q)
 
         rotation["first"] = 0
         quantise_tokens(0)
@@ -434,36 +446,66 @@ def tile_ltransformerdecoderblock_pa_kernel(
         matmuls()
         quantise_tokens(2)
         matmuls()
-        copy_unit((1, 0), 0)
-        copy_unit((1, 0), 1)
         quantise_unit((0, 1))
         quantise_tokens(3)
         quantise_tokens(4)
         open_gate()
 
-        state["sizes"] = [2, 3] * (len(weights) * HALVES - 1) + [2, 2, 1]
         plan = [
-            ((1, 2), (1, 1), [(0, 3), (1, 0), (1, 2)]),
-            ((1, 3), (2, 0), [(1, 1), (1, 3)]),
-            ((2, 2), (2, 1), [(2, 0), (2, 2)]),
-            ((2, 3), None, [(2, 1), (2, 3)]),
+            ((1, 2), (1, 0), None, [(0, 3), (1, 2)], 0),
+            ((1, 1), None, (1, 3), [(1, 0), (1, 1)], 0),
+            ((2, 0), (2, 2), None, [(1, 3), (2, 0)], 0),
+            ((2, 1), (2, 3), None, [(2, 2), (2, 1)], EARLY),
         ]
-        for gpsimd_unit, tensor_unit, ready in plan:
+        for gpsimd_unit, tensor_unit, scalar_unit, ready, early in plan:
             regroup_gpsimd(gpsimd_unit)
+            first = None
+            if early:
+                first = new_slot(early)
+            slot = new_slot(TOKEN_TILES - early)
             for m in range(TOKEN_TILES):
-                if m == TOKEN_TILES - 1 and tensor_unit is not None:
-                    regroup_tensor(tensor_unit)
-                read_bank()
-            for b in range(2):
-                if tensor_unit is not None:
-                    copy_unit(tensor_unit, b)
-            for unit in ready:
-                quantise_unit(unit)
-                matmuls()
+                if m < early:
+                    whole = m == early - 1
+                    read_bank(first, None, (lambda: scalar_square_means(first)) if whole else None)
+                else:
+                    read_bank(slot)
+                if early and m == early + 1:
+                    add_pairs(first)
+                    lift_and_store(first)
+                if m < QUARTERS:
+                    if tensor_unit is not None:
+                        tensor_quarter(tensor_unit, m)
+                    if scalar_unit is not None:
+                        scalar_quarter(scalar_unit, m)
+            quantise_unit(ready[0])
+            matmuls()
+            square_means(slot)
+            quantise_unit(ready[1])
+            sum_heads(slot)
+            matmuls()
             open_gate()
-        state["behind"] = 0
-        while order["read"] < total:
-            read_bank()
-        last = state["due"]
-        sum_heads(last)
-        lift_and_store(last)
+            lift_and_store(slot)
+            if tensor_unit is not None:
+                for b in range(2):
+                    copy_unit(tensor_unit, b)
+
+        due = None
+        for count in LAST:
+            slot = new_slot(count)
+            for j in range(count):
+                if j == 0 and due is not None:
+                    before = due
+                    read_bank(
+                        slot,
+                        lambda: square_means(before),
+                        lambda: (sum_heads(before), lift_and_store(before)),
+                    )
+                else:
+                    read_bank(slot)
+                if order["read"] == 22:
+                    quantise_unit((2, 3))
+                    matmuls()
+            due = slot
+        square_means(due)
+        sum_heads(due)
+        lift_and_store(due)

@@ -10,7 +10,6 @@ U8 = mybir.dt.uint8
 FP8X4 = mybir.dt.float8_e4m3fn_x4
 ACT = mybir.ActivationFunctionType
 ALU = mybir.AluOpType
-AX = mybir.AxisListType
 
 P = 128
 PACK = 4
@@ -30,8 +29,6 @@ HEADS_PER_BANK = N_TILE // HD
 BANKS = 8
 RUN = 4
 QUARTERS = N_TILE // P
-TENSOR_COLS = 1024 // PACK
-EARLY = 3
 LAST = (2, 2, 1, 2, 2, 1)
 AHEAD = 3
 
@@ -76,8 +73,6 @@ def tile_ltransformerdecoderblock_pa_kernel(
 
         ident = consts.tile([P, P], F32)
         make_identity(nc, ident[:])
-        ident_bf = consts.tile([P, P], BF16)
-        nc.vector.tensor_copy(out=ident_bf[:], in_=ident[:])
 
         token = consts.tile([P, 1], F32)
 
@@ -219,7 +214,6 @@ def tile_ltransformerdecoderblock_pa_kernel(
             )
 
         wg = {}
-        turned = {}
         w_codes = {}
         w_scales = {}
         quantised = set()
@@ -246,29 +240,11 @@ def tile_ltransformerdecoderblock_pa_kernel(
                 in_=raw[unit][:, :, cols].rearrange("p t (c i) -> p c t i", i=RUN),
             )
 
-        def tensor_quarter(unit, q):
-            if q == 0:
-                turned[unit] = []
-            if q % 2 == 0:
-                fresh = bank_tile([P, TENSOR_COLS, PACK], BF16)
-                turned[unit].append(fresh)
-            c = q % 2 * P
-            nc.tensor.matmul(
-                out=turned[unit][q // 2][:, c : c + P, :].rearrange("p c t -> p t c"),
-                lhsT=ident_bf[:],
-                rhs=raw[unit][:, :, q * P : (q + 1) * P],
-                start=True,
-                stop=True,
-            )
-
-        def copy_unit(unit, b):
-            if b == 0:
-                wg[unit] = wwork.tile(
-                    [P, N_TILE, PACK], BF16, align_bytes=64, bufs=3, name="wg_t"
-                )
-            nc.scalar.copy(
-                out=wg[unit][:, b * TENSOR_COLS : (b + 1) * TENSOR_COLS, :],
-                in_=turned[unit][b][:],
+        def regroup_vector(unit):
+            wg[unit] = wwork.tile([P, N_TILE, PACK], BF16, align_bytes=64, name="wg_v")
+            nc.vector.tensor_copy(
+                out=wg[unit][:].rearrange("p (c i) t -> p c t i", i=RUN),
+                in_=raw[unit][:, :, :].rearrange("p t (c i) -> p c t i", i=RUN),
             )
 
         def quantise_unit(unit):
@@ -387,19 +363,6 @@ def tile_ltransformerdecoderblock_pa_kernel(
                 in_=slot["lifted"][:].rearrange("p j a c -> p j (a c)"),
             )
 
-        def scalar_square_means(slot):
-            nc.scalar.activation(
-                out=slot["stats"][:, :, :, 1],
-                in_=slot["stats"][:, :, :, 1],
-                func=ACT.Square,
-                scale=float(HD) ** 0.5,
-            )
-
-        def add_pairs(slot):
-            nc.vector.tensor_reduce(
-                out=slot["sumsq"][:], in_=slot["stats"][:, :, :, 1:], op=ALU.add, axis=AX.X
-            )
-
         def read_bank(slot, middle=None, before_copy=None):
             matmuls()
             head_stats(slot, middle)
@@ -452,42 +415,29 @@ def tile_ltransformerdecoderblock_pa_kernel(
         open_gate()
 
         plan = [
-            ((1, 2), (1, 0), None, [(0, 3), (1, 2)], 0),
-            ((1, 1), None, (1, 3), [(1, 0), (1, 1)], 0),
-            ((2, 0), (2, 2), None, [(1, 3), (2, 0)], 0),
-            ((2, 1), (2, 3), None, [(2, 2), (2, 1)], EARLY),
+            ((1, 2), (1, 0), [(0, 3), (1, 2)]),
+            ((1, 1), (1, 3), [(1, 0), (1, 1)]),
+            ((2, 0), (2, 2), [(1, 3), (2, 0)]),
+            ((2, 1), None, [(2, 2), (2, 1)]),
         ]
-        for gpsimd_unit, tensor_unit, scalar_unit, ready, early in plan:
+        for gpsimd_unit, scalar_unit, ready in plan:
             regroup_gpsimd(gpsimd_unit)
-            first = None
-            if early:
-                first = new_slot(early)
-            slot = new_slot(TOKEN_TILES - early)
+            slot = new_slot(TOKEN_TILES)
             for m in range(TOKEN_TILES):
-                if m < early:
-                    whole = m == early - 1
-                    read_bank(first, None, (lambda: scalar_square_means(first)) if whole else None)
-                else:
-                    read_bank(slot)
-                if early and m == early + 1:
-                    add_pairs(first)
-                    lift_and_store(first)
-                if m < QUARTERS:
-                    if tensor_unit is not None:
-                        tensor_quarter(tensor_unit, m)
-                    if scalar_unit is not None:
-                        scalar_quarter(scalar_unit, m)
+                read_bank(slot)
+                if m < QUARTERS and scalar_unit is not None:
+                    scalar_quarter(scalar_unit, m)
             quantise_unit(ready[0])
             matmuls()
             square_means(slot)
             quantise_unit(ready[1])
             sum_heads(slot)
             matmuls()
-            open_gate()
+            if scalar_unit is None:
+                regroup_vector((2, 3))
+            else:
+                open_gate()
             lift_and_store(slot)
-            if tensor_unit is not None:
-                for b in range(2):
-                    copy_unit(tensor_unit, b)
 
         due = None
         for count in LAST:
@@ -502,7 +452,7 @@ def tile_ltransformerdecoderblock_pa_kernel(
                     )
                 else:
                     read_bank(slot)
-                if order["read"] == 22:
+                if order["read"] == total - TOKEN_TILES - AHEAD:
                     quantise_unit((2, 3))
                     matmuls()
             due = slot

@@ -10,6 +10,7 @@ U8 = mybir.dt.uint8
 FP8X4 = mybir.dt.float8_e4m3fn_x4
 ACT = mybir.ActivationFunctionType
 ALU = mybir.AluOpType
+AX = mybir.AxisListType
 
 P = 128
 PACK = 4
@@ -29,7 +30,16 @@ HEADS_PER_BANK = N_TILE // HD
 BANKS = 8
 RUN = 4
 QUARTERS = N_TILE // P
-LAST = (2, 2, 1, 2, 2, 1)
+TENSOR_COLS = 1024 // PACK
+G1 = [(0, 0), (0, 2)]
+S1 = [(0, 1), (0, 3)]
+Q1 = [(0, 1)]
+XV = []
+LAST = [('v', 1), ('v', 2), ('v', 2), ('v', 1)]
+LATE = []
+CARRY = -1
+IDLE = 0
+PLAN = [{'g': (1, 2), 's': [(1, 0)], 'ready': [(0, 3), (1, 2)], 'n': 4}, {'g': (1, 1), 's': [(1, 3)], 'ready': [(1, 0), (1, 1)]}, {'g': (2, 0), 's': [(2, 2)], 'ready': [(1, 3), (2, 0)]}, {'g': (2, 1), 'ready': [(2, 2), (2, 1)]}, {'g': (2, 3), 'ready': [(2, 3)], 'gate': False, 'early': 1}]
 AHEAD = 3
 
 FLOPS = 2 * TOKENS * D * 3 * E
@@ -73,6 +83,8 @@ def tile_ltransformerdecoderblock_pa_kernel(
 
         ident = consts.tile([P, P], F32)
         make_identity(nc, ident[:])
+        ident_bf = consts.tile([P, P], BF16)
+        nc.vector.tensor_copy(out=ident_bf[:], in_=ident[:])
 
         token = consts.tile([P, 1], F32)
 
@@ -135,6 +147,17 @@ def tile_ltransformerdecoderblock_pa_kernel(
             gain_all.append(spread)
 
         sumsq = {}
+        def keep_tensor_busy(unit):
+            for c in range(IDLE):
+                idle = bank_tile([P, N_TILE], F32)
+                nc.tensor.matmul(
+                    out=idle[:],
+                    lhsT=ones[:],
+                    rhs=wg[unit][:, : N_TILE // PACK, :].rearrange("p n t -> p (n t)"),
+                    start=True,
+                    stop=True,
+                )
+
         rms = {}
         rstd = {}
         xt = {}
@@ -194,9 +217,9 @@ def tile_ltransformerdecoderblock_pa_kernel(
                         ident[:],
                     )
 
-        def copy_tokens(m):
+        def copy_tokens(m, copy=nc.scalar.copy):
             xg[m] = consts.tile([P, PASSES, P, PACK], BF16, align_bytes=64, name="xg%d" % m)
-            nc.scalar.copy(
+            copy(
                 out=xg[m][:]
                 .rearrange("p g r t -> p (g r t)")
                 .bitcast(F32)
@@ -214,6 +237,7 @@ def tile_ltransformerdecoderblock_pa_kernel(
             )
 
         wg = {}
+        turned = {}
         w_codes = {}
         w_scales = {}
         quantised = set()
@@ -238,6 +262,31 @@ def tile_ltransformerdecoderblock_pa_kernel(
             nc.scalar.copy(
                 out=wg[unit][:, cols, :].rearrange("p (c i) t -> p c t i", i=RUN),
                 in_=raw[unit][:, :, cols].rearrange("p t (c i) -> p c t i", i=RUN),
+            )
+
+        def tensor_quarter(unit, q):
+            if q == 0:
+                turned[unit] = []
+            if q % 2 == 0:
+                fresh = bank_tile([P, TENSOR_COLS, PACK], BF16)
+                turned[unit].append(fresh)
+            c = q % 2 * P
+            nc.tensor.matmul(
+                out=turned[unit][q // 2][:, c : c + P, :].rearrange("p c t -> p t c"),
+                lhsT=ident_bf[:],
+                rhs=raw[unit][:, :, q * P : (q + 1) * P],
+                start=True,
+                stop=True,
+            )
+
+        def copy_unit(unit, b):
+            if b == 0:
+                wg[unit] = wwork.tile(
+                    [P, N_TILE, PACK], BF16, align_bytes=64, bufs=3, name="wg_t"
+                )
+            nc.scalar.copy(
+                out=wg[unit][:, b * TENSOR_COLS : (b + 1) * TENSOR_COLS, :],
+                in_=turned[unit][b][:],
             )
 
         def regroup_vector(unit):
@@ -354,14 +403,42 @@ def tile_ltransformerdecoderblock_pa_kernel(
                 bias=1.0 / CURV,
             )
             width = HEADS_PER_BANK * (HD + 1)
-            w, m, h = bank_parts(slot["banks"][0])
-            count = len(slot["banks"])
-            nc.sync.dma_start(
-                out=outputs[w][m * P : (m + count) * P, h * width : (h + 1) * width].rearrange(
-                    "(m p) c -> p m c", p=P
-                ),
-                in_=slot["lifted"][:].rearrange("p j a c -> p j (a c)"),
+            j = 0
+            while j < len(slot["banks"]):
+                w, m, h = bank_parts(slot["banks"][j])
+                count = min(len(slot["banks"]) - j, TOKEN_TILES - m)
+                nc.sync.dma_start(
+                    out=outputs[w][
+                        m * P : (m + count) * P, h * width : (h + 1) * width
+                    ].rearrange("(m p) c -> p m c", p=P),
+                    in_=slot["lifted"][:, j : j + count].rearrange("p j a c -> p j (a c)"),
+                )
+                j += count
+
+        def scalar_square_means(slot):
+            nc.scalar.activation(
+                out=slot["stats"][:, :, :, 1],
+                in_=slot["stats"][:, :, :, 1],
+                func=ACT.Square,
+                scale=float(HD) ** 0.5,
             )
+
+        def add_pairs(slot):
+            nc.vector.tensor_reduce(
+                out=slot["sumsq"][:], in_=slot["stats"][:, :, :, 1:], op=ALU.add, axis=AX.X
+            )
+
+        def gpsimd_sums(slot, j):
+            work = opool.tile([P, HEADS_PER_BANK, HD], F32, bufs=2, name="gwork")
+            p = slot["lifted"][:, j, :, 1:]
+            nc.gpsimd.tensor_tensor(out=work[:], in0=p, in1=p, op=ALU.mult)
+            half = HD // 2
+            while half >= 1:
+                target = work[:, :, :half] if half > 1 else slot["sumsq"][:, j, :].unsqueeze(2)
+                nc.gpsimd.tensor_tensor(
+                    out=target, in0=work[:, :, :half], in1=work[:, :, half : 2 * half], op=ALU.add
+                )
+                half //= 2
 
         def read_bank(slot, middle=None, before_copy=None):
             matmuls()
@@ -375,8 +452,8 @@ def tile_ltransformerdecoderblock_pa_kernel(
         root(0)
         sum_squares("vector", 1)
         open_gate()
-        regroup_gpsimd((0, 0))
-        regroup_gpsimd((0, 2))
+        for u in G1[:2]:
+            regroup_gpsimd(u)
         reciprocal(0)
         sum_squares("scalar", 2)
         root(1)
@@ -392,14 +469,18 @@ def tile_ltransformerdecoderblock_pa_kernel(
         root(4)
         copy_tokens(1)
         norm_transpose(3, between=4)
+        for u in G1[2:]:
+            regroup_gpsimd(u)
         copy_tokens(2)
-        for q in range(QUARTERS):
-            scalar_quarter((0, 1), q)
+        for u in S1[:1]:
+            for q in range(QUARTERS):
+                scalar_quarter(u, q)
         norm_transpose(4)
-        copy_tokens(3)
-        copy_tokens(4)
-        for q in range(QUARTERS):
-            scalar_quarter((0, 3), q)
+        for m in (3, 4):
+            copy_tokens(m, nc.vector.tensor_copy if m in XV else nc.scalar.copy)
+        for u in S1[1:]:
+            for q in range(QUARTERS):
+                scalar_quarter(u, q)
 
         rotation["first"] = 0
         quantise_tokens(0)
@@ -409,39 +490,82 @@ def tile_ltransformerdecoderblock_pa_kernel(
         matmuls()
         quantise_tokens(2)
         matmuls()
-        quantise_unit((0, 1))
+        for u in Q1:
+            quantise_unit(u)
         quantise_tokens(3)
         quantise_tokens(4)
         open_gate()
 
-        plan = [
-            ((1, 2), (1, 0), [(0, 3), (1, 2)]),
-            ((1, 1), (1, 3), [(1, 0), (1, 1)]),
-            ((2, 0), (2, 2), [(1, 3), (2, 0)]),
-            ((2, 1), None, [(2, 2), (2, 1)]),
-        ]
-        for gpsimd_unit, scalar_unit, ready in plan:
-            regroup_gpsimd(gpsimd_unit)
-            slot = new_slot(TOKEN_TILES)
-            for m in range(TOKEN_TILES):
-                read_bank(slot)
-                if m < QUARTERS and scalar_unit is not None:
-                    scalar_quarter(scalar_unit, m)
-            quantise_unit(ready[0])
-            matmuls()
+        carry = []
+        for cyc in PLAN:
+            g = cyc.get("g")
+            if g is not None:
+                regroup_gpsimd(g)
+            early = cyc.get("early", 0)
+            first = new_slot(early) if early else None
+            banks = cyc.get("n", TOKEN_TILES)
+            slot = new_slot(banks - early)
+            jobs = [("s", u, q) for u in cyc.get("s", []) for q in range(QUARTERS)]
+            jobs += [("p", u, q) for u in cyc.get("p", []) for q in range(QUARTERS)]
+            at = cyc.get("at", 0)
+            per = cyc.get("per", 1)
+            for m in range(banks):
+                if m < early:
+                    whole = m == early - 1
+                    read_bank(first, None, (lambda: scalar_square_means(first)) if whole else None)
+                else:
+                    read_bank(slot)
+                if carry and m >= CARRY:
+                    lift_and_store(carry.pop(0))
+                if early and m == early + (1 if early < 4 else 0):
+                    add_pairs(first)
+                    lift_and_store(first)
+                if m >= at:
+                    for i in range(per if m < banks - 1 else 99):
+                        if jobs:
+                            k, u, q = jobs.pop(0)
+                            (scalar_quarter if k == "s" else tensor_quarter)(u, q)
+            ready = list(cyc.get("ready", []))
+            if g is not None:
+                keep_tensor_busy(g)
+            if ready:
+                quantise_unit(ready.pop(0))
+                matmuls()
             square_means(slot)
-            quantise_unit(ready[1])
+            if ready:
+                quantise_unit(ready.pop(0))
+                matmuls()
             sum_heads(slot)
+            for u in ready:
+                quantise_unit(u)
             matmuls()
-            if scalar_unit is None:
-                regroup_vector((2, 3))
-            else:
+            if cyc.get("v") is not None:
+                regroup_vector(cyc["v"])
+            if cyc.get("gate", True):
                 open_gate()
-            lift_and_store(slot)
+            for u in cyc.get("p", []):
+                copy_unit(u, 0)
+                copy_unit(u, 1)
+            if CARRY < 0:
+                lift_and_store(slot)
+            else:
+                carry.append(slot)
 
         due = None
-        for count in LAST:
+        pending = []
+        for kind, count in LAST:
             slot = new_slot(count)
+            if kind == "g":
+                for j in range(count):
+                    matmuls()
+                    b = order["read"]
+                    order["read"] += 1
+                    slot["banks"].append(b)
+                    matmuls()
+                    copy_out(slot, j)
+                    gpsimd_sums(slot, j)
+                pending.append(slot)
+                continue
             for j in range(count):
                 if j == 0 and due is not None:
                     before = due
@@ -452,10 +576,18 @@ def tile_ltransformerdecoderblock_pa_kernel(
                     )
                 else:
                     read_bank(slot)
-                if order["read"] == total - TOKEN_TILES - AHEAD:
-                    quantise_unit((2, 3))
-                    matmuls()
+                if carry:
+                    lift_and_store(carry.pop(0))
+                for n, u in LATE:
+                    if order["read"] == n:
+                        if u is None:
+                            lift_and_store(pending.pop(0))
+                        else:
+                            quantise_unit(u)
+                            matmuls()
             due = slot
         square_means(due)
         sum_heads(due)
+        for p in pending:
+            lift_and_store(p)
         lift_and_store(due)

@@ -38,8 +38,9 @@ XV = []
 LAST = [('v', 1), ('v', 2), ('v', 2), ('v', 1)]
 LATE = []
 CARRY = -1
+ROOT1 = 0
 IDLE = 0
-PLAN = [{'g': (1, 2), 's': [(1, 0)], 'ready': [(0, 3), (1, 2)], 'n': 4}, {'g': (1, 1), 's': [(1, 3)], 'ready': [(1, 0), (1, 1)]}, {'g': (2, 0), 's': [(2, 2)], 'ready': [(1, 3), (2, 0)]}, {'g': (2, 1), 'ready': [(2, 2), (2, 1)]}, {'g': (2, 3), 'ready': [(2, 3)], 'gate': False, 'early': 1}]
+PLAN = [{'g': (1, 0), 'ready': [(0, 3), (1, 0)], 'n': 4, 'p': [(1, 2)], 'at': 0}, {'g': (1, 1), 's': [(1, 3)], 'ready': [(1, 2), (1, 1)]}, {'g': (2, 0), 'ready': [(1, 3), (2, 0)], 'p': [(2, 2)], 'at': 0}, {'g': (2, 1), 'ready': [(2, 2), (2, 1)]}, {'g': (2, 3), 'ready': [(2, 3)], 'gate': False, 'early': 1}]
 AHEAD = 3
 
 FLOPS = 2 * TOKENS * D * 3 * E
@@ -296,6 +297,20 @@ def tile_ltransformerdecoderblock_pa_kernel(
                 in_=raw[unit][:, :, :].rearrange("p t (c i) -> p c t i", i=RUN),
             )
 
+        def quantise_half(unit, half):
+            w, u = unit
+            if half == 0:
+                w_codes[unit] = consts.tile([P, N_TILE], U32, name="wc%d_%d" % (w, u), align_bytes=64)
+                w_scales[unit] = consts.tile([P, N_TILE], U8, name="wsc%d_%d" % (w, u), align_bytes=64)
+            cols = slice(half * N_TILE // 2, (half + 1) * N_TILE // 2)
+            nc.vector.quantize_mx(
+                out=w_codes[unit][:, cols].bitcast(FP8X4),
+                scales=w_scales[unit][:, cols],
+                in_=wg[unit][:, cols, :].rearrange("p n t -> p (n t)"),
+            )
+            if half == 1:
+                quantised.add(unit)
+
         def quantise_unit(unit):
             w, u = unit
             w_codes[unit] = consts.tile([P, N_TILE], U32, name="wc%d_%d" % (w, u), align_bytes=64)
@@ -371,8 +386,8 @@ def tile_ltransformerdecoderblock_pa_kernel(
                     ),
                 )
 
-        def copy_out(slot, j):
-            nc.scalar.copy(
+        def copy_out(slot, j, copy=nc.scalar.copy):
+            copy(
                 out=slot["lifted"][:, j, :, 1:],
                 in_=acc[slot["banks"][j]][:].rearrange("p (a c) -> p a c", c=HD),
             )
@@ -440,25 +455,33 @@ def tile_ltransformerdecoderblock_pa_kernel(
                 )
                 half //= 2
 
-        def read_bank(slot, middle=None, before_copy=None):
+        def read_bank(slot, middle=None, before_copy=None, copy=nc.scalar.copy):
             matmuls()
             head_stats(slot, middle)
             matmuls()
             if before_copy is not None:
                 before_copy()
-            copy_out(slot, len(slot["banks"]) - 1)
+            copy_out(slot, len(slot["banks"]) - 1, copy)
 
         sum_squares("scalar", 0)
         root(0)
         sum_squares("vector", 1)
+        if ROOT1:
+            reciprocal(0)
         open_gate()
         for u in G1[:2]:
             regroup_gpsimd(u)
-        reciprocal(0)
-        sum_squares("scalar", 2)
-        root(1)
-        norm_transpose(0)
-        reciprocal(1)
+        if not ROOT1:
+            reciprocal(0)
+        if ROOT1:
+            root(1)
+            sum_squares("scalar", 2)
+            norm_transpose(0, between=1)
+        else:
+            sum_squares("scalar", 2)
+            root(1)
+            norm_transpose(0)
+            reciprocal(1)
         sum_squares("scalar", 3)
         root(2)
         norm_transpose(1, between=2)
@@ -514,7 +537,7 @@ def tile_ltransformerdecoderblock_pa_kernel(
                     whole = m == early - 1
                     read_bank(first, None, (lambda: scalar_square_means(first)) if whole else None)
                 else:
-                    read_bank(slot)
+                    read_bank(slot, None, None, nc.vector.tensor_copy if m in cyc.get("vc", []) else nc.scalar.copy)
                 if carry and m >= CARRY:
                     lift_and_store(carry.pop(0))
                 if early and m == early + (1 if early < 4 else 0):
@@ -528,13 +551,20 @@ def tile_ltransformerdecoderblock_pa_kernel(
             ready = list(cyc.get("ready", []))
             if g is not None:
                 keep_tensor_busy(g)
-            if ready:
-                quantise_unit(ready.pop(0))
+            if len(ready) == 1:
+                quantise_half(ready[0], 0)
+                square_means(slot)
+                quantise_half(ready[0], 1)
                 matmuls()
-            square_means(slot)
-            if ready:
-                quantise_unit(ready.pop(0))
-                matmuls()
+                ready = []
+            else:
+                if ready:
+                    quantise_unit(ready.pop(0))
+                    matmuls()
+                square_means(slot)
+                if ready:
+                    quantise_unit(ready.pop(0))
+                    matmuls()
             sum_heads(slot)
             for u in ready:
                 quantise_unit(u)

@@ -229,8 +229,8 @@ def tile_ltransformerdecoderblock_pa_kernel(
             )
 
         def quantise_tokens(m):
-            x_codes[m] = consts.tile([P, PASSES * P], U32, name="xc%d" % m, align_bytes=64)
-            x_scales[m] = consts.tile([P, PASSES * P], U8, name="xsc%d" % m, align_bytes=64)
+            x_codes[m] = consts.tile([P, PASSES * P], U32, name="xc%d" % m, align_bytes=256)
+            x_scales[m] = consts.tile([P, PASSES * P], U8, name="xsc%d" % m, align_bytes=256)
             nc.vector.quantize_mx(
                 out=x_codes[m][:].bitcast(FP8X4),
                 scales=x_scales[m][:],
@@ -300,8 +300,8 @@ def tile_ltransformerdecoderblock_pa_kernel(
         def quantise_half(unit, half):
             w, u = unit
             if half == 0:
-                w_codes[unit] = consts.tile([P, N_TILE], U32, name="wc%d_%d" % (w, u), align_bytes=64)
-                w_scales[unit] = consts.tile([P, N_TILE], U8, name="wsc%d_%d" % (w, u), align_bytes=64)
+                w_codes[unit] = consts.tile([P, N_TILE], U32, name="wc%d_%d" % (w, u), align_bytes=256)
+                w_scales[unit] = consts.tile([P, N_TILE], U8, name="wsc%d_%d" % (w, u), align_bytes=256)
             cols = slice(half * N_TILE // 2, (half + 1) * N_TILE // 2)
             nc.vector.quantize_mx(
                 out=w_codes[unit][:, cols].bitcast(FP8X4),
@@ -313,8 +313,8 @@ def tile_ltransformerdecoderblock_pa_kernel(
 
         def quantise_unit(unit):
             w, u = unit
-            w_codes[unit] = consts.tile([P, N_TILE], U32, name="wc%d_%d" % (w, u), align_bytes=64)
-            w_scales[unit] = consts.tile([P, N_TILE], U8, name="wsc%d_%d" % (w, u), align_bytes=64)
+            w_codes[unit] = consts.tile([P, N_TILE], U32, name="wc%d_%d" % (w, u), align_bytes=256)
+            w_scales[unit] = consts.tile([P, N_TILE], U8, name="wsc%d_%d" % (w, u), align_bytes=256)
             nc.vector.quantize_mx(
                 out=w_codes[unit][:].bitcast(FP8X4),
                 scales=w_scales[unit][:],
@@ -410,7 +410,7 @@ def tile_ltransformerdecoderblock_pa_kernel(
                 op1=ALU.add,
             )
 
-        def lift_and_store(slot):
+        def lift_and_store(slot, queue=nc.sync):
             nc.scalar.activation(
                 out=slot["lifted"][:, :, :, 0],
                 in_=slot["sumsq"][:],
@@ -422,7 +422,7 @@ def tile_ltransformerdecoderblock_pa_kernel(
             while j < len(slot["banks"]):
                 w, m, h = bank_parts(slot["banks"][j])
                 count = min(len(slot["banks"]) - j, TOKEN_TILES - m)
-                nc.sync.dma_start(
+                queue.dma_start(
                     out=outputs[w][
                         m * P : (m + count) * P, h * width : (h + 1) * width
                     ].rearrange("(m p) c -> p m c", p=P),
@@ -620,4 +620,4 @@ def tile_ltransformerdecoderblock_pa_kernel(
         sum_heads(due)
         for p in pending:
             lift_and_store(p)
-        lift_and_store(due)
+        lift_and_store(due, nc.scalar)

from contextlib import ExitStack

import concourse.mybir as mybir
from concourse.masks import make_identity

F32 = mybir.dt.float32
BF16 = mybir.dt.bfloat16
U32 = mybir.dt.uint32
U8 = mybir.dt.uint8
FP8X4 = mybir.dt.float8_e4m3fn_x4
ACT = mybir.ActivationFunctionType
ALU = mybir.AluOpType
AX = mybir.AxisListType

P = 128
PACK = 4
K_PASS = P * PACK
TOKENS = 2 * 320
D = 1024
E = 1024
H = 16
HD = 64
EPS = 1e-6
CURV = 1.0
PASSES = D // K_PASS
TOKEN_TILES = TOKENS // P
N_TILE = 512
HALVES = E // N_TILE
HEADS_PER_BANK = N_TILE // HD
BANKS = 8
RUN = 4
QUARTERS = N_TILE // P
TENSOR_COLS = 1024 // PACK
G1 = [(0, 0), (0, 2)]
S1 = [(0, 1), (0, 3)]
Q1 = [(0, 1)]
XV = []
LAST = [('v', 1), ('v', 2), ('v', 2), ('v', 1)]
LATE = []
CARRY = -1
ROOT1 = 0
IDLE = 0
PLAN = [{'g': (1, 0), 'ready': [(0, 3), (1, 0)], 'n': 4, 'p': [(1, 2)], 'at': 0}, {'g': (1, 1), 's': [(1, 3)], 'ready': [(1, 2), (1, 1)]}, {'g': (2, 0), 'ready': [(1, 3), (2, 0)], 'p': [(2, 2)], 'at': 0}, {'g': (2, 1), 'ready': [(2, 2), (2, 1)]}, {'g': (2, 3), 'ready': [(2, 3)], 'gate': False, 'early': 1}]
AHEAD = 3

FLOPS = 2 * TOKENS * D * 3 * E


def tile_ltransformerdecoderblock_pa_kernel(
    tc, x_space, ln1_w, wq, wk, wv, out_0, out_1, out_2
):
    nc = tc.nc
    weights = (wq, wk, wv)
    outputs = [o.rearrange("b s h c -> (b s) (h c)") for o in (out_0, out_1, out_2)]
    x_rows = x_space.flatten_outer_dims()

    with ExitStack() as ctx:
        consts = ctx.enter_context(tc.tile_pool(name="consts", bufs=1))
        xwork = ctx.enter_context(tc.tile_pool(name="xwork", bufs=3))
        wwork = ctx.enter_context(tc.tile_pool(name="wwork", bufs=2))
        opool = ctx.enter_context(tc.tile_pool(name="opool", bufs=1))
        psum = ctx.enter_context(tc.psum_pool(name="psum", bufs=1))
        ctx.enter_context(tc.manual_schedule())

        rotation = {"next": 0, "first": 2}

        def bank_tile(shape, dtype):
            b = rotation["next"]
            if b < rotation["first"]:
                b = rotation["first"]
            rotation["next"] = (b + 1) % BANKS
            fresh = psum.tile(shape, dtype, tag="bank%d" % b, name="bank%d" % b)
            return fresh

        one = consts.tile([P, 1], F32)
        nc.vector.memset(one[:], 1.0)
        warm = consts.tile([P, 1], F32)
        nc.scalar.activation(out=warm[:], in_=one[:], func=ACT.Sqrt)

        gain_row = consts.tile([P, D], BF16)
        nc.gpsimd.memset(gain_row[:].bitcast(F32), 0.0)
        ones = consts.tile([P, P], BF16)
        nc.vector.memset(ones[:], 1.0)

        ident = consts.tile([P, P], F32)
        make_identity(nc, ident[:])
        ident_bf = consts.tile([P, P], BF16)
        nc.vector.tensor_copy(out=ident_bf[:], in_=ident[:])

        token = consts.tile([P, 1], F32)

        def open_gate():
            nc.vector.memset(token[:], 1.0)

        x_sb = []
        raw = {}

        def load_tokens(m):
            x_tile = consts.tile([P, D], BF16, name="x%d" % m)
            nc.sync.dma_start(out=x_tile[:], in_=x_rows[m * P : (m + 1) * P, :])
            x_sb.append(x_tile)

        def load_unit(w, u):
            g, h = divmod(u, HALVES)
            raw[(w, u)] = consts.tile([P, PACK, N_TILE], BF16, name="raw%d_%d" % (w, u))
            nc.sync.dma_start(
                out=raw[(w, u)][:],
                in_=weights[w][
                    g * K_PASS : (g + 1) * K_PASS, h * N_TILE : (h + 1) * N_TILE
                ].rearrange("(p j) n -> p j n", j=PACK),
            )

        def load_chunk(w, g):
            raw_tile = consts.tile([P, PACK, E], BF16, name="raw%d_g%d" % (w, g))
            nc.sync.dma_start(
                out=raw_tile[:],
                in_=weights[w][g * K_PASS : (g + 1) * K_PASS, :].rearrange(
                    "(p j) n -> p j n", j=PACK
                ),
            )
            for h in range(HALVES):
                raw[(w, g * HALVES + h)] = raw_tile[:, :, h * N_TILE : (h + 1) * N_TILE]

        load_tokens(0)
        nc.sync.dma_start(out=gain_row[0:1, :], in_=ln1_w.rearrange("(o d) -> o d", o=1))
        load_tokens(1)
        load_tokens(2)
        load_unit(0, 0)
        load_tokens(3)
        load_tokens(4)
        load_unit(0, 2)
        load_unit(0, 1)
        load_unit(0, 3)
        for w in range(1, len(weights)):
            for g in range(PASSES):
                load_chunk(w, g)

        gain_all = []
        for h in range(D // N_TILE):
            spread = psum.tile([P, N_TILE], F32, tag="bank%d" % h, name="spread%d" % h)
            nc.tensor.matmul(
                out=spread[:],
                lhsT=ones[:],
                rhs=gain_row[:, h * N_TILE : (h + 1) * N_TILE],
                start=True,
                stop=True,
            )
            gain_all.append(spread)

        sumsq = {}
        def keep_tensor_busy(unit):
            for c in range(IDLE):
                idle = bank_tile([P, N_TILE], F32)
                nc.tensor.matmul(
                    out=idle[:],
                    lhsT=ones[:],
                    rhs=wg[unit][:, : N_TILE // PACK, :].rearrange("p n t -> p (n t)"),
                    start=True,
                    stop=True,
                )

        rms = {}
        rstd = {}
        xt = {}
        xg = {}
        x_codes = {}
        x_scales = {}

        def sum_squares(engine, m):
            squares = xwork.tile([P, D], BF16, name="squares")
            sumsq[m] = consts.tile([P, 1], F32, name="sumsq%d" % m)
            if engine == "scalar":
                nc.scalar.activation(
                    out=squares[:], in_=x_sb[m][:], func=ACT.Square, accum_out=sumsq[m][:]
                )
            else:
                nc.vector.scalar_tensor_tensor(
                    out=squares[:],
                    in0=x_sb[m][:],
                    scalar=1.0,
                    in1=x_sb[m][:],
                    op0=ALU.mult,
                    op1=ALU.mult,
                    accum_out=sumsq[m][:],
                )

        def root(m):
            rms[m] = consts.tile([P, 1], F32, name="rms%d" % m)
            nc.scalar.activation(
                out=rms[m][:], in_=sumsq[m][:], func=ACT.Sqrt, scale=1.0 / D, bias=EPS
            )

        def reciprocal(m):
            rstd[m] = consts.tile([P, 1], F32, name="rstd%d" % m)
            nc.vector.reciprocal(out=rstd[m][:], in_=rms[m][:])

        def norm_transpose(m, between=None):
            normed = xwork.tile([P, D], BF16, name="normed")
            for h in range(D // N_TILE):
                cols = slice(h * N_TILE, (h + 1) * N_TILE)
                nc.vector.scalar_tensor_tensor(
                    out=normed[:, cols],
                    in0=x_sb[m][:, cols],
                    scalar=rstd[m][:],
                    in1=gain_all[h][:],
                    op0=ALU.mult,
                    op1=ALU.mult,
                )
                if h == 0 and between is not None:
                    reciprocal(between)
            words = normed[:].bitcast(F32)
            xt[m] = bank_tile([P, PASSES, 2, P], F32)
            for g in range(PASSES):
                for u in range(2):
                    nc.tensor.transpose(
                        xt[m][:, g, u, :],
                        words[:, g * 2 * P + u : (g + 1) * 2 * P : 2],
                        ident[:],
                    )

        def copy_tokens(m, copy=nc.scalar.copy):
            xg[m] = consts.tile([P, PASSES, P, PACK], BF16, align_bytes=64, name="xg%d" % m)
            copy(
                out=xg[m][:]
                .rearrange("p g r t -> p (g r t)")
                .bitcast(F32)
                .rearrange("p (g r u) -> p g r u", g=PASSES, u=2),
                in_=xt[m][:].rearrange("p g u r -> p g r u"),
            )

        def quantise_tokens(m):
            x_codes[m] = consts.tile([P, PASSES * P], U32, name="xc%d" % m, align_bytes=256)
            x_scales[m] = consts.tile([P, PASSES * P], U8, name="xsc%d" % m, align_bytes=256)
            nc.vector.quantize_mx(
                out=x_codes[m][:].bitcast(FP8X4),
                scales=x_scales[m][:],
                in_=xg[m][:].rearrange("p g r t -> p (g r t)"),
            )

        wg = {}
        turned = {}
        w_codes = {}
        w_scales = {}
        quantised = set()

        def regroup_gpsimd(unit):
            wg[unit] = wwork.tile([P, N_TILE, PACK], BF16, align_bytes=64, name="wg_g")
            nc.gpsimd.tensor_scalar(
                out=wg[unit][:],
                in0=raw[unit][:, :, :].rearrange("p t c -> p c t"),
                scalar1=token[:],
                scalar2=0.0,
                op0=ALU.mult,
                op1=ALU.add,
            )

        def scalar_quarter(unit, q):
            if q == 0:
                wg[unit] = wwork.tile(
                    [P, N_TILE, PACK], BF16, align_bytes=64, bufs=3, name="wg_s"
                )
            cols = slice(q * P, (q + 1) * P)
            nc.scalar.copy(
                out=wg[unit][:, cols, :].rearrange("p (c i) t -> p c t i", i=RUN),
                in_=raw[unit][:, :, cols].rearrange("p t (c i) -> p c t i", i=RUN),
            )

        def tensor_quarter(unit, q):
            if q == 0:
                turned[unit] = []
            if q % 2 == 0:
                fresh = bank_tile([P, TENSOR_COLS, PACK], BF16)
                turned[unit].append(fresh)
            c = q % 2 * P
            nc.tensor.matmul(
                out=turned[unit][q // 2][:, c : c + P, :].rearrange("p c t -> p t c"),
                lhsT=ident_bf[:],
                rhs=raw[unit][:, :, q * P : (q + 1) * P],
                start=True,
                stop=True,
            )

        def copy_unit(unit, b):
            if b == 0:
                wg[unit] = wwork.tile(
                    [P, N_TILE, PACK], BF16, align_bytes=64, bufs=3, name="wg_t"
                )
            nc.scalar.copy(
                out=wg[unit][:, b * TENSOR_COLS : (b + 1) * TENSOR_COLS, :],
                in_=turned[unit][b][:],
            )

        def regroup_vector(unit):
            wg[unit] = wwork.tile([P, N_TILE, PACK], BF16, align_bytes=64, name="wg_v")
            nc.vector.tensor_copy(
                out=wg[unit][:].rearrange("p (c i) t -> p c t i", i=RUN),
                in_=raw[unit][:, :, :].rearrange("p t (c i) -> p c t i", i=RUN),
            )

        def quantise_half(unit, half):
            w, u = unit
            if half == 0:
                w_codes[unit] = consts.tile([P, N_TILE], U32, name="wc%d_%d" % (w, u), align_bytes=256)
                w_scales[unit] = consts.tile([P, N_TILE], U8, name="wsc%d_%d" % (w, u), align_bytes=256)
            cols = slice(half * N_TILE // 2, (half + 1) * N_TILE // 2)
            nc.vector.quantize_mx(
                out=w_codes[unit][:, cols].bitcast(FP8X4),
                scales=w_scales[unit][:, cols],
                in_=wg[unit][:, cols, :].rearrange("p n t -> p (n t)"),
            )
            if half == 1:
                quantised.add(unit)

        def quantise_unit(unit):
            w, u = unit
            w_codes[unit] = consts.tile([P, N_TILE], U32, name="wc%d_%d" % (w, u), align_bytes=256)
            w_scales[unit] = consts.tile([P, N_TILE], U8, name="wsc%d_%d" % (w, u), align_bytes=256)
            nc.vector.quantize_mx(
                out=w_codes[unit][:].bitcast(FP8X4),
                scales=w_scales[unit][:],
                in_=wg[unit][:].rearrange("p n t -> p (n t)"),
            )
            quantised.add(unit)

        def bank_parts(b):
            i, m = divmod(b, TOKEN_TILES)
            w, h = divmod(i, HALVES)
            return w, m, h

        total = len(weights) * HALVES * TOKEN_TILES
        filled = []
        acc = {}
        order = {"filled": 0, "read": 0}

        def matmuls():
            while order["filled"] < min(order["read"] + AHEAD, total):
                b = order["filled"]
                w, m, h = bank_parts(b)
                if m not in x_codes or any(
                    (w, g * HALVES + h) not in quantised for g in range(PASSES)
                ):
                    return
                order["filled"] += 1
                acc[b] = bank_tile([P, N_TILE], F32)
                for g in range(PASSES):
                    nc.tensor.matmul_mx(
                        out=acc[b][:],
                        lhsT=x_codes[m][:, g * P : (g + 1) * P].bitcast(FP8X4),
                        lhsT_scale=x_scales[m][:, g * P : (g + 1) * P],
                        rhs=w_codes[(w, g * HALVES + h)][:].bitcast(FP8X4),
                        rhs_scale=w_scales[(w, g * HALVES + h)][:],
                        start=(g == 0),
                        stop=(g == PASSES - 1),
                    )

        slots = []

        def new_slot(count):
            s = len(slots)
            slots.append(
                {
                    "count": count,
                    "banks": [],
                    "lifted": opool.tile(
                        [P, count, HEADS_PER_BANK, HD + 1], F32, name="lifted%d" % s
                    ),
                    "stats": opool.tile([P, count, HEADS_PER_BANK, 3], F32, name="stats%d" % s),
                    "mean_sq": opool.tile([P, count, HEADS_PER_BANK], F32, name="mean_sq%d" % s),
                    "sumsq": opool.tile([P, count, HEADS_PER_BANK], F32, name="sumsq_h%d" % s),
                }
            )
            return slots[s]

        def head_stats(slot, middle=None):
            b = order["read"]
            order["read"] += 1
            j = len(slot["banks"])
            slot["banks"].append(b)
            for q in range(HEADS_PER_BANK // 2):
                if q == HEADS_PER_BANK // 4 and middle is not None:
                    middle()
                nc.vector.bn_stats(
                    out=slot["stats"][:, j, 2 * q : 2 * q + 2, :].rearrange("p a s -> p (a s)"),
                    in_=acc[b][:, 2 * q * HD : (2 * q + 2) * HD].rearrange(
                        "p (a c) -> p c a", a=2
                    ),
                )

        def copy_out(slot, j, copy=nc.scalar.copy):
            copy(
                out=slot["lifted"][:, j, :, 1:],
                in_=acc[slot["banks"][j]][:].rearrange("p (a c) -> p a c", c=HD),
            )

        def square_means(slot):
            nc.vector.tensor_tensor(
                out=slot["mean_sq"][:],
                in0=slot["stats"][:, :, :, 1],
                in1=slot["stats"][:, :, :, 1],
                op=ALU.mult,
            )

        def sum_heads(slot):
            nc.vector.scalar_tensor_tensor(
                out=slot["sumsq"][:],
                in0=slot["mean_sq"][:],
                scalar=float(HD),
                in1=slot["stats"][:, :, :, 2],
                op0=ALU.mult,
                op1=ALU.add,
            )

        def lift_and_store(slot, queue=nc.sync):
            nc.scalar.activation(
                out=slot["lifted"][:, :, :, 0],
                in_=slot["sumsq"][:],
                func=ACT.Sqrt,
                bias=1.0 / CURV,
            )
            width = HEADS_PER_BANK * (HD + 1)
            j = 0
            while j < len(slot["banks"]):
                w, m, h = bank_parts(slot["banks"][j])
                count = min(len(slot["banks"]) - j, TOKEN_TILES - m)
                queue.dma_start(
                    out=outputs[w][
                        m * P : (m + count) * P, h * width : (h + 1) * width
                    ].rearrange("(m p) c -> p m c", p=P),
                    in_=slot["lifted"][:, j : j + count].rearrange("p j a c -> p j (a c)"),
                )
                j += count

        def scalar_square_means(slot):
            nc.scalar.activation(
                out=slot["stats"][:, :, :, 1],
                in_=slot["stats"][:, :, :, 1],
                func=ACT.Square,
                scale=float(HD) ** 0.5,
            )

        def add_pairs(slot):
            nc.vector.tensor_reduce(
                out=slot["sumsq"][:], in_=slot["stats"][:, :, :, 1:], op=ALU.add, axis=AX.X
            )

        def gpsimd_sums(slot, j):
            work = opool.tile([P, HEADS_PER_BANK, HD], F32, bufs=2, name="gwork")
            p = slot["lifted"][:, j, :, 1:]
            nc.gpsimd.tensor_tensor(out=work[:], in0=p, in1=p, op=ALU.mult)
            half = HD // 2
            while half >= 1:
                target = work[:, :, :half] if half > 1 else slot["sumsq"][:, j, :].unsqueeze(2)
                nc.gpsimd.tensor_tensor(
                    out=target, in0=work[:, :, :half], in1=work[:, :, half : 2 * half], op=ALU.add
                )
                half //= 2

        def read_bank(slot, middle=None, before_copy=None, copy=nc.scalar.copy):
            matmuls()
            head_stats(slot, middle)
            matmuls()
            if before_copy is not None:
                before_copy()
            copy_out(slot, len(slot["banks"]) - 1, copy)

        sum_squares("scalar", 0)
        root(0)
        sum_squares("vector", 1)
        if ROOT1:
            reciprocal(0)
        open_gate()
        for u in G1[:2]:
            regroup_gpsimd(u)
        if not ROOT1:
            reciprocal(0)
        if ROOT1:
            root(1)
            sum_squares("scalar", 2)
            norm_transpose(0, between=1)
        else:
            sum_squares("scalar", 2)
            root(1)
            norm_transpose(0)
            reciprocal(1)
        sum_squares("scalar", 3)
        root(2)
        norm_transpose(1, between=2)
        sum_squares("scalar", 4)
        root(3)
        copy_tokens(0)
        norm_transpose(2, between=3)
        root(4)
        copy_tokens(1)
        norm_transpose(3, between=4)
        for u in G1[2:]:
            regroup_gpsimd(u)
        copy_tokens(2)
        for u in S1[:1]:
            for q in range(QUARTERS):
                scalar_quarter(u, q)
        norm_transpose(4)
        for m in (3, 4):
            copy_tokens(m, nc.vector.tensor_copy if m in XV else nc.scalar.copy)
        for u in S1[1:]:
            for q in range(QUARTERS):
                scalar_quarter(u, q)

        rotation["first"] = 0
        quantise_tokens(0)
        quantise_unit((0, 0))
        quantise_tokens(1)
        quantise_unit((0, 2))
        matmuls()
        quantise_tokens(2)
        matmuls()
        for u in Q1:
            quantise_unit(u)
        quantise_tokens(3)
        quantise_tokens(4)
        open_gate()

        carry = []
        for cyc in PLAN:
            g = cyc.get("g")
            if g is not None:
                regroup_gpsimd(g)
            early = cyc.get("early", 0)
            first = new_slot(early) if early else None
            banks = cyc.get("n", TOKEN_TILES)
            slot = new_slot(banks - early)
            jobs = [("s", u, q) for u in cyc.get("s", []) for q in range(QUARTERS)]
            jobs += [("p", u, q) for u in cyc.get("p", []) for q in range(QUARTERS)]
            at = cyc.get("at", 0)
            per = cyc.get("per", 1)
            for m in range(banks):
                if m < early:
                    whole = m == early - 1
                    read_bank(first, None, (lambda: scalar_square_means(first)) if whole else None)
                else:
                    read_bank(slot, None, None, nc.vector.tensor_copy if m in cyc.get("vc", []) else nc.scalar.copy)
                if carry and m >= CARRY:
                    lift_and_store(carry.pop(0))
                if early and m == early + (1 if early < 4 else 0):
                    add_pairs(first)
                    lift_and_store(first)
                if m >= at:
                    for i in range(per if m < banks - 1 else 99):
                        if jobs:
                            k, u, q = jobs.pop(0)
                            (scalar_quarter if k == "s" else tensor_quarter)(u, q)
            ready = list(cyc.get("ready", []))
            if g is not None:
                keep_tensor_busy(g)
            if len(ready) == 1:
                quantise_half(ready[0], 0)
                square_means(slot)
                quantise_half(ready[0], 1)
                matmuls()
                ready = []
            else:
                if ready:
                    quantise_unit(ready.pop(0))
                    matmuls()
                square_means(slot)
                if ready:
                    quantise_unit(ready.pop(0))
                    matmuls()
            sum_heads(slot)
            for u in ready:
                quantise_unit(u)
            matmuls()
            if cyc.get("v") is not None:
                regroup_vector(cyc["v"])
            if cyc.get("gate", True):
                open_gate()
            for u in cyc.get("p", []):
                copy_unit(u, 0)
                copy_unit(u, 1)
            if CARRY < 0:
                lift_and_store(slot)
            else:
                carry.append(slot)

        due = None
        pending = []
        for kind, count in LAST:
            slot = new_slot(count)
            if kind == "g":
                for j in range(count):
                    matmuls()
                    b = order["read"]
                    order["read"] += 1
                    slot["banks"].append(b)
                    matmuls()
                    copy_out(slot, j)
                    gpsimd_sums(slot, j)
                pending.append(slot)
                continue
            for j in range(count):
                if j == 0 and due is not None:
                    before = due
                    read_bank(
                        slot,
                        lambda: square_means(before),
                        lambda: (sum_heads(before), lift_and_store(before)),
                    )
                else:
                    read_bank(slot)
                if carry:
                    lift_and_store(carry.pop(0))
                for n, u in LATE:
                    if order["read"] == n:
                        if u is None:
                            lift_and_store(pending.pop(0))
                        else:
                            quantise_unit(u)
                            matmuls()
            due = slot
        square_means(due)
        sum_heads(due)
        for p in pending:
            lift_and_store(p)
        lift_and_store(due, nc.scalar)
